import numpy as np
import ml_dtypes


def mxq(x, axis, fmt="e4m3"):
    dtype, down = {"e4m3": (ml_dtypes.float8_e4m3fn, 7), "e5m2": (ml_dtypes.float8_e5m2, 14)}[fmt]
    v = np.moveaxis(np.asarray(x, np.float32).astype(ml_dtypes.bfloat16).astype(np.float64), axis, -1)
    blocks = v.reshape(v.shape[:-1] + (-1, 32))
    amax = np.abs(blocks).max(-1, keepdims=True)
    byte = np.maximum(np.where(amax > 0, np.frexp(amax)[1] - 1 + 127, 0) - down, 1)
    scale = np.exp2(byte - 127.0)
    codes = (blocks / scale).astype(np.float32).astype(dtype).astype(np.float64)
    return np.moveaxis((codes * scale).reshape(v.shape), -1, axis)


WIDE = False


def mx_kscale(k):
    if not WIDE:
        return np.ones(k)
    levels = np.array([10, -10, 5, -5, 0])
    a = np.random.permutation(np.resize(levels, k // 512 * 4)).reshape(k // 512, 4)
    idx = np.arange(k)
    return np.exp2(a[idx // 512, idx % 128 // 32])


BF16 = ml_dtypes.bfloat16


def bf(x):
    return np.asarray(x, np.float32).astype(BF16)


def f64(x):
    return np.asarray(x).astype(np.float64)


B, I, H = 512, 1024, 1024
FORGET_GATE_BIAS = -1.0
EPS = 1e-5


def sigmoid(v):
    return 1.0 / (1.0 + np.exp(-v))


def layer_norm_1d(x, weight, bias):
    mean = np.mean(x, axis=1, keepdims=True)
    std = np.std(x, axis=1, keepdims=True, ddof=1)
    return (x - mean) / (std + EPS) * weight + bias


def setup_inputs():
    s, t = mx_kscale(I), mx_kscale(H)
    return {
        "inputs": bf(np.random.standard_normal((B, I)) * s),
        "hx": bf(np.random.standard_normal((B, H)) * t),
        "cx": bf(np.random.standard_normal((B, H))),
        "w_i2h": bf(np.random.standard_normal((4 * H, I)) / np.sqrt(I) / s),
        "b_i2h": bf(np.random.standard_normal(4 * H) * 0.3),
        "w_h2h": bf(np.random.standard_normal((4 * H, H)) / np.sqrt(H) / t),
        "b_h2h": bf(np.random.standard_normal(4 * H) * 0.3),
        "ln_i2h_w": bf(1.0 + 0.2 * np.random.standard_normal((1, 4 * H))),
        "ln_i2h_b": bf(0.2 * np.random.standard_normal((1, 4 * H))),
        "ln_h2h_w": bf(1.0 + 0.2 * np.random.standard_normal((1, 4 * H))),
        "ln_h2h_b": bf(0.2 * np.random.standard_normal((1, 4 * H))),
        "ln_h2o_w": bf(1.0 + 0.2 * np.random.standard_normal((1, H))),
        "ln_h2o_b": bf(0.2 * np.random.standard_normal((1, H))),
    }


def reference(inputs, hx, cx, w_i2h, b_i2h, w_h2h, b_h2h,
              ln_i2h_w, ln_i2h_b, ln_h2h_w, ln_h2h_b, ln_h2o_w, ln_h2o_b):
    i2h = (mxq(f64(inputs), 1, "e4m3") @ mxq(f64(w_i2h), 1, "e4m3").T) + f64(b_i2h)
    h2h = (mxq(f64(hx), 1, "e4m3") @ mxq(f64(w_h2h), 1, "e4m3").T) + f64(b_h2h)
    x = layer_norm_1d(i2h, f64(ln_i2h_w), f64(ln_i2h_b)) + layer_norm_1d(h2h, f64(ln_h2h_w), f64(ln_h2h_b))
    g_i, g_f, g_o, g_c = np.split(x, 4, axis=1)
    in_gate = sigmoid(g_i)
    forget_gate = sigmoid(g_f + FORGET_GATE_BIAS)
    out_gate = sigmoid(g_o)
    in_transform = np.tanh(g_c)
    cx_new = forget_gate * f64(cx) + in_gate * in_transform
    hx_new = out_gate * np.tanh(layer_norm_1d(cx_new, f64(ln_h2o_w), f64(ln_h2o_b)))
    return hx_new, cx_new

@@ -1,0 +1,299 @@
+from contextlib import ExitStack
+
+import concourse.bass as bass
+import concourse.masks as masks
+import concourse.mybir as mybir
+import concourse.tile as tile
+
+F32 = mybir.dt.float32
+BF16 = mybir.dt.bfloat16
+U32 = mybir.dt.uint32
+U8 = mybir.dt.uint8
+I32 = mybir.dt.int32
+FP8X4 = mybir.dt.float8_e4m3fn_x4
+ALU = mybir.AluOpType
+ACT = mybir.ActivationFunctionType
+AX = mybir.AxisListType
+
+P = 128
+B = 512
+K = 1024
+H = 1024
+G4 = 4 * H
+RT = B // P
+CH = 512
+NCH = G4 // CH
+EPS = 1e-5
+
+FLOPS = 2 * 2 * B * K * G4
+
+
+def tile_layernormlstmcell_kernel(
+    tc, inputs, hx, cx, w_i2h, b_i2h, w_h2h, b_h2h,
+    ln_i2h_w, ln_i2h_b, ln_h2h_w, ln_h2h_b, ln_h2o_w, ln_h2o_b, out_0, out_1,
+):
+    nc = tc.nc
+    acts = [inputs, hx]
+    weights = [w_i2h, w_h2h]
+    biases = [b_i2h, b_h2h]
+    ln_w = [ln_i2h_w, ln_h2h_w]
+    ln_b = [ln_i2h_b, ln_h2h_b]
+
+    with ExitStack() as ctx:
+        const = ctx.enter_context(tc.tile_pool(name="const", bufs=1))
+        stage = ctx.enter_context(tc.tile_pool(name="stage", bufs=2))
+        psum = ctx.enter_context(tc.psum_pool(name="psum", bufs=4))
+
+        ident_f = const.tile([P, P], F32, name="ident_f")
+        masks.make_identity(nc, ident_f[:])
+        ident_b = const.tile([P, P], BF16, name="ident_b")
+        masks.make_identity(nc, ident_b[:])
+
+        krhs = const.tile([P, G4], BF16, name="krhs")
+        nc.vector.memset(krhs[:].bitcast(I32), 0)
+        coef = const.tile([P, RT, P], BF16, name="coef")
+        nc.vector.memset(coef[:], 0.0)
+        nc.vector.memset(coef[:, :, 6:8], 1.0)
+        half = const.tile([P, RT], F32, name="half")
+        nc.vector.memset(half[:], 0.5)
+        negone = const.tile([P, 1], F32, name="negone")
+        nc.vector.memset(negone[:], -1.0)
+
+        acodes = [const.tile([P, 2 * B], U32, name="acodes%d" % m, align_bytes=64) for m in range(2)]
+        ascales = [const.tile([P, 2 * B], U8, name="ascales%d" % m, align_bytes=64) for m in range(2)]
+        v = [[const.tile([P, G4], F32, name="v%d_%d" % (m, r)) for r in range(RT)] for m in range(2)]
+        wbc = [const.tile([P, G4], BF16, name="wbc%d" % m) for m in range(2)]
+        w3bc = const.tile([P, H], BF16, name="w3bc")
+        b3bc = const.tile([P, H], BF16, name="b3bc")
+        cx_sb = const.tile([P, RT, H], BF16, name="cx_sb")
+        coefT = const.tile([P, RT * P], BF16, name="coefT")
+
+        sums = const.tile([P, 2 * RT * NCH], F32, name="sums")
+        sqs = const.tile([P, 2 * RT * NCH], F32, name="sqs")
+        shift = [const.tile([P, RT], F32, name="shift%d" % m) for m in range(2)]
+        rinv = [const.tile([P, RT], F32, name="rinv%d" % m) for m in range(2)]
+
+        def prep(rows, codes, scales):
+            raw = stage.tile([P, 4, K], BF16, tag="raw", bufs=3, name="raw")
+            nc.sync.dma_start(out=raw[:], in_=rows.rearrange("(t p) k -> p t k", p=P))
+            grouped = stage.tile([P, 2048], F32, tag="grouped", name="grouped", align_bytes=64)
+            gview = grouped[:].rearrange("p (g j u) -> p g j u", g=2, u=2)
+            for g in range(2):
+                for hf in range(2):
+                    tp = psum.tile([P, 2, 256], F32, tag="tp", name="tp")
+                    for u in range(2):
+                        for tt in range(2):
+                            q = 2 * g + u
+                            nc.tensor.transpose(
+                                tp[:, u, tt * P:(tt + 1) * P],
+                                raw[:, 2 * hf + tt, :].bitcast(F32)[:, q * P:(q + 1) * P],
+                                ident_f[:],
+                            )
+                    if g == 1 and hf == 1:
+                        nc.vector.tensor_copy(
+                            out=gview[:, g, hf * 256:(hf + 1) * 256, :],
+                            in_=tp[:].rearrange("p u j -> p j u"),
+                        )
+                    else:
+                        nc.scalar.copy(
+                            out=gview[:, g, hf * 256:(hf + 1) * 256, :],
+                            in_=tp[:].rearrange("p u j -> p j u"),
+                        )
+            for g in range(2):
+                nc.vector.quantize_mx(
+                    out=codes[:, g * 512:(g + 1) * 512].bitcast(FP8X4),
+                    scales=scales[:, g * 512:(g + 1) * 512],
+                    in_=grouped[:, g * 1024:(g + 1) * 1024].bitcast(BF16),
+                )
+
+        def prep_w(idx):
+            m, c = divmod(idx, NCH)
+            wcodes = stage.tile([P, 1024], U32, tag="wcodes", name="wcodes", align_bytes=64)
+            wscales = stage.tile([P, 1024], U8, tag="wscales", name="wscales", align_bytes=64)
+            prep(weights[m][c * CH:(c + 1) * CH, :], wcodes, wscales)
+            bbc = stage.tile([P, CH], BF16, tag="bbc", bufs=3, name="bbc")
+            nc.sync.dma_start(out=bbc[:], in_=biases[m][c * CH:(c + 1) * CH].partition_broadcast(P))
+            return wcodes, wscales, bbc
+
+        def work(idx, ops):
+            m, c = divmod(idx, NCH)
+            wcodes, wscales, bbc = ops
+            cols = slice(c * CH, (c + 1) * CH)
+            for r in range(RT):
+                acc = psum.tile([P, CH], F32, tag="acc", name="acc")
+                for g in range(2):
+                    a_cols = slice(g * B + r * P, g * B + (r + 1) * P)
+                    w_cols = slice(g * CH, (g + 1) * CH)
+                    nc.tensor.matmul_mx(
+                        out=acc[:],
+                        lhsT=acodes[m][:, a_cols].bitcast(FP8X4),
+                        lhsT_scale=ascales[m][:, a_cols],
+                        rhs=wcodes[:, w_cols].bitcast(FP8X4),
+                        rhs_scale=wscales[:, w_cols],
+                        start=(g == 0),
+                        stop=(g == 1),
+                    )
+                k = (m * RT + r) * NCH + c
+                nc.vector.scalar_tensor_tensor(
+                    out=v[m][r][:, cols], in0=acc[:], scalar=1.0, in1=bbc[:],
+                    op0=ALU.mult, op1=ALU.add, accum_out=sums[:, k:k + 1],
+                )
+            if c == 0:
+                first = sums[:, m * RT * NCH:(m + 1) * RT * NCH].rearrange("p (r c) -> p r c", c=NCH)[:, :, 0]
+                nc.vector.tensor_scalar(
+                    out=shift[m][:], in0=first, scalar1=-1.0 / CH, scalar2=None, op0=ALU.mult,
+                )
+            for r in range(RT):
+                k = (m * RT + r) * NCH + c
+                junk = stage.tile([P, CH], BF16, tag="junk", name="junk")
+                nc.scalar.activation(
+                    out=junk[:], in_=v[m][r][:, cols], func=ACT.Square,
+                    bias=shift[m][:, r:r + 1], scale=1.0, accum_out=sqs[:, k:k + 1],
+                )
+                nc.gpsimd.tensor_tensor(
+                    out=v[m][r][:, cols], in0=v[m][r][:, cols], in1=wbc[m][:, cols], op=ALU.mult,
+                )
+
+        def small(name):
+            return const.tile([P, RT], F32, name=name)
+
+        cview = coef[:, :, 0:6].rearrange("p r (l s) -> p r l s", s=3)
+
+        def stats(m):
+            n = float(G4)
+            seg = slice(m * RT * NCH, (m + 1) * RT * NCH)
+            s1 = small("s1_%d" % m)
+            nc.vector.tensor_reduce(out=s1[:], in_=sums[:, seg].rearrange("p (r c) -> p r c", c=NCH), axis=AX.X, op=ALU.add)
+            q1 = small("q1_%d" % m)
+            nc.vector.tensor_reduce(out=q1[:], in_=sqs[:, seg].rearrange("p (r c) -> p r c", c=NCH), axis=AX.X, op=ALU.add)
+            mean = small("mean_%d" % m)
+            nc.vector.tensor_scalar(out=mean[:], in0=s1[:], scalar1=1.0 / n, scalar2=None, op0=ALU.mult)
+            d = small("d_%d" % m)
+            nc.vector.tensor_tensor(out=d[:], in0=mean[:], in1=shift[m][:], op=ALU.add)
+            d2 = small("d2_%d" % m)
+            nc.vector.scalar_tensor_tensor(out=d2[:], in0=d[:], scalar=n, in1=d[:], op0=ALU.mult, op1=ALU.mult)
+            var = small("var_%d" % m)
+            nc.vector.tensor_tensor(out=var[:], in0=q1[:], in1=d2[:], op=ALU.subtract)
+            nc.vector.tensor_scalar(out=var[:], in0=var[:], scalar1=1.0 / (n - 1.0), scalar2=0.0, op0=ALU.mult, op1=ALU.max)
+            std = small("std_%d" % m)
+            nc.gpsimd.tensor_tensor(out=std[:], in0=var[:], in1=half[:], op=ALU.pow)
+            nc.vector.tensor_scalar(out=std[:], in0=std[:], scalar1=EPS, scalar2=None, op0=ALU.add)
+            nc.vector.reciprocal(out=rinv[m][:], in_=std[:])
+            alpha = small("alpha_%d" % m)
+            nc.vector.scalar_tensor_tensor(out=alpha[:], in0=mean[:], scalar=-1.0, in1=rinv[m][:], op0=ALU.mult, op1=ALU.mult)
+            nc.vector.tensor_copy(out=cview[:, :, m, 0], in_=alpha[:])
+            rem = small("rem_%d" % m)
+            nc.vector.tensor_tensor(out=rem[:], in0=alpha[:], in1=cview[:, :, m, 0], op=ALU.subtract)
+            nc.vector.tensor_copy(out=cview[:, :, m, 1], in_=rem[:])
+            rem2 = small("rem2_%d" % m)
+            nc.vector.tensor_tensor(out=rem2[:], in0=rem[:], in1=cview[:, :, m, 1], op=ALU.subtract)
+            nc.vector.tensor_copy(out=cview[:, :, m, 2], in_=rem2[:])
+
+        prep(acts[0], acodes[0], ascales[0])
+        nxt = prep_w(0)
+        for m in range(2):
+            nc.sync.dma_start(out=krhs[3 * m:3 * m + 3, :], in_=ln_w[m].rearrange("o n -> (o n)").partition_broadcast(3))
+            nc.sync.dma_start(out=krhs[6 + m:7 + m, :], in_=ln_b[m])
+        nc.sync.dma_start(out=wbc[0][:], in_=ln_w[0].rearrange("o n -> (o n)").partition_broadcast(P))
+        for idx in range(2 * NCH):
+            cur = nxt
+            if idx == 3:
+                nc.sync.dma_start(out=wbc[1][:], in_=ln_w[1].rearrange("o n -> (o n)").partition_broadcast(P))
+            if idx == NCH - 2:
+                prep(acts[1], acodes[1], ascales[1])
+            if idx == NCH + 2:
+                nc.sync.dma_start(out=cx_sb[:], in_=cx.rearrange("(r p) h -> p r h", p=P))
+                nc.sync.dma_start(out=w3bc[:], in_=ln_h2o_w.rearrange("o n -> (o n)").partition_broadcast(P))
+                nc.sync.dma_start(out=b3bc[:], in_=ln_h2o_b.rearrange("o n -> (o n)").partition_broadcast(P))
+            if idx + 1 < 2 * NCH:
+                nxt = prep_w(idx + 1)
+            work(idx, cur)
+            if idx == NCH:
+                stats(0)
+        stats(1)
+
+        ctp = psum.tile([P, RT * P], BF16, tag="tp", name="ctp")
+        for r in range(RT):
+            nc.tensor.transpose(ctp[:, r * P:(r + 1) * P], coef[:, r, :], ident_b[:])
+        nc.scalar.copy(out=coefT[:], in_=ctp[:])
+
+        s3 = const.tile([P, RT], F32, name="s3")
+        q3 = const.tile([P, RT], F32, name="q3")
+        negm3 = const.tile([P, RT], F32, name="negm3")
+        r3 = const.tile([P, RT], F32, name="r3")
+
+        def parts(r):
+            x = v[0][r]
+            tmp = v[1][r]
+            return (x[:, 0:H], x[:, H:2 * H], x[:, 2 * H:3 * H], x[:, 3 * H:4 * H],
+                    tmp[:, 0:H], tmp[:, H:2 * H], tmp[:, 2 * H:3 * H], tmp[:, 3 * H:4 * H])
+
+        def zstep(r):
+            x = v[0][r]
+            for n in range(NCH):
+                cols = slice(n * CH, (n + 1) * CH)
+                kp = psum.tile([P, CH], F32, tag=("acc" if n % 2 == 0 else "tp"), name="kp")
+                nc.tensor.matmul(out=kp[:], lhsT=coefT[:, r * P:(r + 1) * P], rhs=krhs[:, cols], start=True, stop=True)
+                nc.vector.scalar_tensor_tensor(
+                    out=x[:, cols], in0=x[:, cols], scalar=rinv[0][:, r:r + 1], in1=kp[:],
+                    op0=ALU.mult, op1=ALU.add,
+                )
+
+        def xstep(r):
+            x = v[0][r]
+            tmp = v[1][r]
+            for gate in (1, 0, 3, 2):
+                cols = slice(gate * H, (gate + 1) * H)
+                nc.vector.scalar_tensor_tensor(
+                    out=x[:, cols], in0=tmp[:, cols], scalar=rinv[1][:, r:r + 1], in1=x[:, cols],
+                    op0=ALU.mult, op1=ALU.add,
+                )
+
+        def gates(r):
+            gi, gf, go, gc, t0, t1, cn, hn = parts(r)
+            nc.scalar.activation(out=gf, in_=gf, func=ACT.Sigmoid, bias=negone[:, 0:1], scale=1.0)
+            nc.scalar.activation(out=gi, in_=gi, func=ACT.Sigmoid)
+            nc.scalar.activation(out=gc, in_=gc, func=ACT.Tanh)
+            nc.scalar.activation(out=go, in_=go, func=ACT.Sigmoid)
+
+        def ab(r):
+            gi, gf, go, gc, t0, t1, cn, hn = parts(r)
+            eng = nc.gpsimd if r < RT - 1 else nc.vector
+            eng.tensor_tensor(out=t0, in0=gf, in1=cx_sb[:, r, :], op=ALU.mult)
+            eng.tensor_tensor(out=t1, in0=gi, in1=gc, op=ALU.mult)
+
+        def c3(r):
+            gi, gf, go, gc, t0, t1, cn, hn = parts(r)
+            rr = slice(r, r + 1)
+            nc.vector.scalar_tensor_tensor(out=cn, in0=t0, scalar=1.0, in1=t1, op0=ALU.mult, op1=ALU.add, accum_out=s3[:, rr])
+            nc.sync.dma_start(out=out_1[r * P:(r + 1) * P, :], in_=cn)
+            nc.vector.tensor_scalar(out=negm3[:, rr], in0=s3[:, rr], scalar1=-1.0 / H, scalar2=None, op0=ALU.mult)
+            nc.scalar.activation(out=t0, in_=cn, func=ACT.Square, bias=negm3[:, rr], scale=1.0, accum_out=q3[:, rr])
+            nc.vector.scalar_tensor_tensor(out=t1, in0=cn, scalar=negm3[:, rr], in1=w3bc[:], op0=ALU.add, op1=ALU.mult)
+
+        def fin1(r):
+            gi, gf, go, gc, t0, t1, cn, hn = parts(r)
+            rr = slice(r, r + 1)
+            var3 = const.tile([P, 1], F32, name="var3_%d" % r)
+            std3 = const.tile([P, 1], F32, name="std3_%d" % r)
+            nc.vector.tensor_scalar(out=var3[:], in0=q3[:, rr], scalar1=1.0 / (H - 1.0), scalar2=None, op0=ALU.mult)
+            nc.gpsimd.tensor_tensor(out=std3[:], in0=var3[:], in1=half[:, 0:1], op=ALU.pow)
+            nc.vector.tensor_scalar(out=var3[:], in0=std3[:], scalar1=EPS, scalar2=None, op0=ALU.add)
+            nc.vector.reciprocal(out=r3[:, rr], in_=var3[:])
+            nc.vector.scalar_tensor_tensor(out=t1, in0=t1, scalar=r3[:, rr], in1=b3bc[:], op0=ALU.mult, op1=ALU.add)
+            nc.scalar.activation(out=t1, in_=t1, func=ACT.Tanh)
+
+        def fin2(r):
+            gi, gf, go, gc, t0, t1, cn, hn = parts(r)
+            nc.vector.tensor_tensor(out=hn, in0=go, in1=t1, op=ALU.mult)
+            nc.sync.dma_start(out=out_0[r * P:(r + 1) * P, :], in_=hn)
+
+        order = [
+            (zstep, 0), (zstep, 1), (xstep, 0), (gates, 0),
+            (zstep, 2), (xstep, 1), (ab, 0), (gates, 1), (c3, 0),
+            (zstep, 3), (xstep, 2), (ab, 1), (fin1, 0), (gates, 2), (c3, 1), (fin2, 0),
+            (xstep, 3), (ab, 2), (fin1, 1), (gates, 3), (c3, 2), (fin2, 1),
+            (ab, 3), (fin1, 2), (c3, 3), (fin2, 2), (fin1, 3), (fin2, 3),
+        ]
+        for step, r in order:
+            step(r)

@@ -73,6 +73,36 @@ def tile_layernormlstmcell_kernel(
         shift = [const.tile([P, RT], F32, name="shift%d" % m) for m in range(2)]
         rinv = [const.tile([P, RT], F32, name="rinv%d" % m) for m in range(2)]
 
+        vr = const.tile([P, P], BF16, name="vr")
+        nc.scalar.dma_start(out=vr[0:32, :], in_=b_i2h.rearrange("(t j) -> t j", j=P))
+        nc.scalar.dma_start(out=vr[32:64, :], in_=b_h2h.rearrange("(t j) -> t j", j=P))
+        nc.scalar.dma_start(out=vr[64:96, :], in_=ln_i2h_w.rearrange("o (t j) -> (o t) j", j=P))
+        nc.scalar.dma_start(out=vr[96:128, :], in_=ln_h2h_w.rearrange("o (t j) -> (o t) j", j=P))
+        vr2 = const.tile([P, P], BF16, name="vr2")
+        nc.vector.memset(vr2[:], 0.0)
+        nc.scalar.dma_start(out=vr2[0:8, :], in_=ln_h2o_w.rearrange("o (t j) -> (o t) j", j=P))
+        nc.scalar.dma_start(out=vr2[8:16, :], in_=ln_h2o_b.rearrange("o (t j) -> (o t) j", j=P))
+        vc = const.tile([P, P], BF16, name="vc")
+        vc2 = const.tile([P, P], BF16, name="vc2")
+        for src, dst in ((vr, vc), (vr2, vc2)):
+            vps = psum.tile([P, P], BF16, tag="tp", name="vps")
+            nc.tensor.transpose(vps[:], src[:], ident_b[:])
+            nc.vector.tensor_copy(out=dst[:], in_=vps[:])
+
+        def spread(dst, cols, q0, ntiles, eng):
+            bps = psum.tile([P, ntiles * P], BF16, tag="tp", name="bps")
+            for t in range(ntiles):
+                nc.tensor.transpose(
+                    bps[:, t * P:(t + 1) * P], cols[:, q0 + t:q0 + t + 1].to_broadcast([P, P]), ident_b[:],
+                )
+            if eng == "scalar":
+                nc.scalar.copy(out=dst, in_=bps[:])
+            else:
+                nc.vector.tensor_copy(out=dst, in_=bps[:])
+
+        for qq in range(4):
+            spread(wbc[0][:, qq * 1024:(qq + 1) * 1024], vc, 64 + 8 * qq, 8, "vector")
+
         def prep(rows, codes, scales):
             raw = stage.tile([P, 4, K], BF16, tag="raw", bufs=3, name="raw")
             nc.sync.dma_start(out=raw[:], in_=rows.rearrange("(t p) k -> p t k", p=P))
@@ -112,7 +142,7 @@ def tile_layernormlstmcell_kernel(
             wscales = stage.tile([P, 1024], U8, tag="wscales", name="wscales", align_bytes=64)
             prep(weights[m][c * CH:(c + 1) * CH, :], wcodes, wscales)
             bbc = stage.tile([P, CH], BF16, tag="bbc", bufs=3, name="bbc")
-            nc.sync.dma_start(out=bbc[:], in_=biases[m][c * CH:(c + 1) * CH].partition_broadcast(P))
+            spread(bbc[:], vc, 32 * m + 4 * c, 4, "scalar")
             return wcodes, wscales, bbc
 
         def work(idx, ops):
@@ -192,19 +222,19 @@ def tile_layernormlstmcell_kernel(
         prep(acts[0], acodes[0], ascales[0])
         nxt = prep_w(0)
         for m in range(2):
-            nc.sync.dma_start(out=krhs[3 * m:3 * m + 3, :], in_=ln_w[m].rearrange("o n -> (o n)").partition_broadcast(3))
-            nc.sync.dma_start(out=krhs[6 + m:7 + m, :], in_=ln_b[m])
-        nc.sync.dma_start(out=wbc[0][:], in_=ln_w[0].rearrange("o n -> (o n)").partition_broadcast(P))
+            nc.scalar.dma_start(out=krhs[3 * m:3 * m + 3, :], in_=ln_w[m].rearrange("o n -> (o n)").partition_broadcast(3))
+            nc.scalar.dma_start(out=krhs[6 + m:7 + m, :], in_=ln_b[m])
         for idx in range(2 * NCH):
             cur = nxt
             if idx == 3:
-                nc.sync.dma_start(out=wbc[1][:], in_=ln_w[1].rearrange("o n -> (o n)").partition_broadcast(P))
+                for qq in range(4):
+                    spread(wbc[1][:, qq * 1024:(qq + 1) * 1024], vc, 96 + 8 * qq, 8, "vector")
             if idx == NCH - 2:
                 prep(acts[1], acodes[1], ascales[1])
             if idx == NCH + 2:
                 nc.sync.dma_start(out=cx_sb[:], in_=cx.rearrange("(r p) h -> p r h", p=P))
-                nc.sync.dma_start(out=w3bc[:], in_=ln_h2o_w.rearrange("o n -> (o n)").partition_broadcast(P))
-                nc.sync.dma_start(out=b3bc[:], in_=ln_h2o_b.rearrange("o n -> (o n)").partition_broadcast(P))
+                spread(w3bc[:], vc2, 0, 8, "vector")
+                spread(b3bc[:], vc2, 8, 8, "vector")
             if idx + 1 < 2 * NCH:
                 nxt = prep_w(idx + 1)
             work(idx, cur)

@@ -73,36 +73,6 @@ def tile_layernormlstmcell_kernel(
         shift = [const.tile([P, RT], F32, name="shift%d" % m) for m in range(2)]
         rinv = [const.tile([P, RT], F32, name="rinv%d" % m) for m in range(2)]
 
-        vr = const.tile([P, P], BF16, name="vr")
-        nc.scalar.dma_start(out=vr[0:32, :], in_=b_i2h.rearrange("(t j) -> t j", j=P))
-        nc.scalar.dma_start(out=vr[32:64, :], in_=b_h2h.rearrange("(t j) -> t j", j=P))
-        nc.scalar.dma_start(out=vr[64:96, :], in_=ln_i2h_w.rearrange("o (t j) -> (o t) j", j=P))
-        nc.scalar.dma_start(out=vr[96:128, :], in_=ln_h2h_w.rearrange("o (t j) -> (o t) j", j=P))
-        vr2 = const.tile([P, P], BF16, name="vr2")
-        nc.vector.memset(vr2[:], 0.0)
-        nc.scalar.dma_start(out=vr2[0:8, :], in_=ln_h2o_w.rearrange("o (t j) -> (o t) j", j=P))
-        nc.scalar.dma_start(out=vr2[8:16, :], in_=ln_h2o_b.rearrange("o (t j) -> (o t) j", j=P))
-        vc = const.tile([P, P], BF16, name="vc")
-        vc2 = const.tile([P, P], BF16, name="vc2")
-        for src, dst in ((vr, vc), (vr2, vc2)):
-            vps = psum.tile([P, P], BF16, tag="tp", name="vps")
-            nc.tensor.transpose(vps[:], src[:], ident_b[:])
-            nc.vector.tensor_copy(out=dst[:], in_=vps[:])
-
-        def spread(dst, cols, q0, ntiles, eng):
-            bps = psum.tile([P, ntiles * P], BF16, tag="tp", name="bps")
-            for t in range(ntiles):
-                nc.tensor.transpose(
-                    bps[:, t * P:(t + 1) * P], cols[:, q0 + t:q0 + t + 1].to_broadcast([P, P]), ident_b[:],
-                )
-            if eng == "scalar":
-                nc.scalar.copy(out=dst, in_=bps[:])
-            else:
-                nc.vector.tensor_copy(out=dst, in_=bps[:])
-
-        for qq in range(4):
-            spread(wbc[0][:, qq * 1024:(qq + 1) * 1024], vc, 64 + 8 * qq, 8, "vector")
-
         def prep(rows, codes, scales):
             raw = stage.tile([P, 4, K], BF16, tag="raw", bufs=3, name="raw")
             nc.sync.dma_start(out=raw[:], in_=rows.rearrange("(t p) k -> p t k", p=P))
@@ -119,7 +89,7 @@ def tile_layernormlstmcell_kernel(
                                 raw[:, 2 * hf + tt, :].bitcast(F32)[:, q * P:(q + 1) * P],
                                 ident_f[:],
                             )
-                    if g == 1 and hf == 1:
+                    if g == 2:
                         nc.vector.tensor_copy(
                             out=gview[:, g, hf * 256:(hf + 1) * 256, :],
                             in_=tp[:].rearrange("p u j -> p j u"),
@@ -142,7 +112,7 @@ def tile_layernormlstmcell_kernel(
             wscales = stage.tile([P, 1024], U8, tag="wscales", name="wscales", align_bytes=64)
             prep(weights[m][c * CH:(c + 1) * CH, :], wcodes, wscales)
             bbc = stage.tile([P, CH], BF16, tag="bbc", bufs=3, name="bbc")
-            spread(bbc[:], vc, 32 * m + 4 * c, 4, "scalar")
+            nc.sync.dma_start(out=bbc[:], in_=biases[m][c * CH:(c + 1) * CH].partition_broadcast(P))
             return wcodes, wscales, bbc
 
         def work(idx, ops):
@@ -180,7 +150,7 @@ def tile_layernormlstmcell_kernel(
                     out=junk[:], in_=v[m][r][:, cols], func=ACT.Square,
                     bias=shift[m][:, r:r + 1], scale=1.0, accum_out=sqs[:, k:k + 1],
                 )
-                nc.gpsimd.tensor_tensor(
+                nc.vector.tensor_tensor(
                     out=v[m][r][:, cols], in0=v[m][r][:, cols], in1=wbc[m][:, cols], op=ALU.mult,
                 )
 
@@ -222,19 +192,19 @@ def tile_layernormlstmcell_kernel(
         prep(acts[0], acodes[0], ascales[0])
         nxt = prep_w(0)
         for m in range(2):
-            nc.scalar.dma_start(out=krhs[3 * m:3 * m + 3, :], in_=ln_w[m].rearrange("o n -> (o n)").partition_broadcast(3))
-            nc.scalar.dma_start(out=krhs[6 + m:7 + m, :], in_=ln_b[m])
+            nc.sync.dma_start(out=krhs[3 * m:3 * m + 3, :], in_=ln_w[m].rearrange("o n -> (o n)").partition_broadcast(3))
+            nc.sync.dma_start(out=krhs[6 + m:7 + m, :], in_=ln_b[m])
+        nc.sync.dma_start(out=wbc[0][:], in_=ln_w[0].rearrange("o n -> (o n)").partition_broadcast(P))
         for idx in range(2 * NCH):
             cur = nxt
             if idx == 3:
-                for qq in range(4):
-                    spread(wbc[1][:, qq * 1024:(qq + 1) * 1024], vc, 96 + 8 * qq, 8, "vector")
+                nc.sync.dma_start(out=wbc[1][:], in_=ln_w[1].rearrange("o n -> (o n)").partition_broadcast(P))
             if idx == NCH - 2:
                 prep(acts[1], acodes[1], ascales[1])
             if idx == NCH + 2:
                 nc.sync.dma_start(out=cx_sb[:], in_=cx.rearrange("(r p) h -> p r h", p=P))
-                spread(w3bc[:], vc2, 0, 8, "vector")
-                spread(b3bc[:], vc2, 8, 8, "vector")
+                nc.sync.dma_start(out=w3bc[:], in_=ln_h2o_w.rearrange("o n -> (o n)").partition_broadcast(P))
+                nc.sync.dma_start(out=b3bc[:], in_=ln_h2o_b.rearrange("o n -> (o n)").partition_broadcast(P))
             if idx + 1 < 2 * NCH:
                 nxt = prep_w(idx + 1)
             work(idx, cur)
@@ -288,7 +258,7 @@ def tile_layernormlstmcell_kernel(
 
         def ab(r):
             gi, gf, go, gc, t0, t1, cn, hn = parts(r)
-            eng = nc.gpsimd if r < RT - 1 else nc.vector
+            eng = nc.vector
             eng.tensor_tensor(out=t0, in0=gf, in1=cx_sb[:, r, :], op=ALU.mult)
             eng.tensor_tensor(out=t1, in0=gi, in1=gc, op=ALU.mult)
 

@@ -1,15 +1,12 @@
 from contextlib import ExitStack
 
-import concourse.bass as bass
 import concourse.masks as masks
 import concourse.mybir as mybir
-import concourse.tile as tile
 
 F32 = mybir.dt.float32
 BF16 = mybir.dt.bfloat16
 U32 = mybir.dt.uint32
 U8 = mybir.dt.uint8
-I32 = mybir.dt.int32
 FP8X4 = mybir.dt.float8_e4m3fn_x4
 ALU = mybir.AluOpType
 ACT = mybir.ActivationFunctionType
@@ -36,8 +33,6 @@ def tile_layernormlstmcell_kernel(
     acts = [inputs, hx]
     weights = [w_i2h, w_h2h]
     biases = [b_i2h, b_h2h]
-    ln_w = [ln_i2h_w, ln_h2h_w]
-    ln_b = [ln_i2h_b, ln_h2h_b]
 
     with ExitStack() as ctx:
         const = ctx.enter_context(tc.tile_pool(name="const", bufs=1))
@@ -49,11 +44,6 @@ def tile_layernormlstmcell_kernel(
         ident_b = const.tile([P, P], BF16, name="ident_b")
         masks.make_identity(nc, ident_b[:])
 
-        krhs = const.tile([P, G4], BF16, name="krhs")
-        nc.vector.memset(krhs[:].bitcast(I32), 0)
-        coef = const.tile([P, RT, P], BF16, name="coef")
-        nc.vector.memset(coef[:], 0.0)
-        nc.vector.memset(coef[:, :, 6:8], 1.0)
         half = const.tile([P, RT], F32, name="half")
         nc.vector.memset(half[:], 0.5)
         negone = const.tile([P, 1], F32, name="negone")
@@ -61,17 +51,29 @@ def tile_layernormlstmcell_kernel(
 
         acodes = [const.tile([P, 2 * B], U32, name="acodes%d" % m, align_bytes=64) for m in range(2)]
         ascales = [const.tile([P, 2 * B], U8, name="ascales%d" % m, align_bytes=64) for m in range(2)]
-        v = [[const.tile([P, G4], F32, name="v%d_%d" % (m, r)) for r in range(RT)] for m in range(2)]
-        wbc = [const.tile([P, G4], BF16, name="wbc%d" % m) for m in range(2)]
+        va = [const.tile([P, RT, G4], F32, name="va%d" % m) for m in range(2)]
         w3bc = const.tile([P, H], BF16, name="w3bc")
         b3bc = const.tile([P, H], BF16, name="b3bc")
         cx_sb = const.tile([P, RT, H], BF16, name="cx_sb")
-        coefT = const.tile([P, RT * P], BF16, name="coefT")
 
         sums = const.tile([P, 2 * RT * NCH], F32, name="sums")
         sqs = const.tile([P, 2 * RT * NCH], F32, name="sqs")
         shift = [const.tile([P, RT], F32, name="shift%d" % m) for m in range(2)]
         rinv = [const.tile([P, RT], F32, name="rinv%d" % m) for m in range(2)]
+        negmean = [const.tile([P, RT], F32, name="negmean%d" % m) for m in range(2)]
+        nbias = [const.tile([P, RT], F32, name="nbias%d" % m) for m in range(2)]
+
+        vr = const.tile([P, P], BF16, name="vr")
+        nc.scalar.dma_start(out=vr[0:32, :], in_=ln_i2h_w.rearrange("o (t j) -> (o t) j", j=P))
+        nc.scalar.dma_start(out=vr[32:64, :], in_=ln_h2h_w.rearrange("o (t j) -> (o t) j", j=P))
+        nc.scalar.dma_start(out=vr[64:96, :], in_=ln_i2h_b.rearrange("o (t j) -> (o t) j", j=P))
+        nc.scalar.dma_start(out=vr[96:128, :], in_=ln_h2h_b.rearrange("o (t j) -> (o t) j", j=P))
+        vps = psum.tile([P, P], BF16, tag="tp", name="vps")
+        nc.tensor.transpose(vps[:], vr[:], ident_b[:])
+        vcf = const.tile([P, P], F32, name="vcf")
+        nc.vector.tensor_copy(out=vcf[:], in_=vps[:])
+        lbc = const.tile([P, 32], F32, name="lbc")
+        nc.vector.tensor_tensor(out=lbc[:], in0=vcf[:, 64:96], in1=vcf[:, 96:128], op=ALU.add)
 
         def prep(rows, codes, scales):
             raw = stage.tile([P, 4, K], BF16, tag="raw", bufs=3, name="raw")
@@ -89,7 +91,7 @@ def tile_layernormlstmcell_kernel(
                                 raw[:, 2 * hf + tt, :].bitcast(F32)[:, q * P:(q + 1) * P],
                                 ident_f[:],
                             )
-                    if g == 2:
+                    if g == 1 and hf == 1:
                         nc.vector.tensor_copy(
                             out=gview[:, g, hf * 256:(hf + 1) * 256, :],
                             in_=tp[:].rearrange("p u j -> p j u"),
@@ -135,7 +137,7 @@ def tile_layernormlstmcell_kernel(
                     )
                 k = (m * RT + r) * NCH + c
                 nc.vector.scalar_tensor_tensor(
-                    out=v[m][r][:, cols], in0=acc[:], scalar=1.0, in1=bbc[:],
+                    out=va[m][:, r, cols], in0=acc[:], scalar=1.0, in1=bbc[:],
                     op0=ALU.mult, op1=ALU.add, accum_out=sums[:, k:k + 1],
                 )
             if c == 0:
@@ -147,17 +149,12 @@ def tile_layernormlstmcell_kernel(
                 k = (m * RT + r) * NCH + c
                 junk = stage.tile([P, CH], BF16, tag="junk", name="junk")
                 nc.scalar.activation(
-                    out=junk[:], in_=v[m][r][:, cols], func=ACT.Square,
+                    out=junk[:], in_=va[m][:, r, cols], func=ACT.Square,
                     bias=shift[m][:, r:r + 1], scale=1.0, accum_out=sqs[:, k:k + 1],
-                )
-                nc.vector.tensor_tensor(
-                    out=v[m][r][:, cols], in0=v[m][r][:, cols], in1=wbc[m][:, cols], op=ALU.mult,
                 )
 
         def small(name):
             return const.tile([P, RT], F32, name=name)
-
-        cview = coef[:, :, 0:6].rearrange("p r (l s) -> p r l s", s=3)
 
         def stats(m):
             n = float(G4)
@@ -166,10 +163,9 @@ def tile_layernormlstmcell_kernel(
             nc.vector.tensor_reduce(out=s1[:], in_=sums[:, seg].rearrange("p (r c) -> p r c", c=NCH), axis=AX.X, op=ALU.add)
             q1 = small("q1_%d" % m)
             nc.vector.tensor_reduce(out=q1[:], in_=sqs[:, seg].rearrange("p (r c) -> p r c", c=NCH), axis=AX.X, op=ALU.add)
-            mean = small("mean_%d" % m)
-            nc.vector.tensor_scalar(out=mean[:], in0=s1[:], scalar1=1.0 / n, scalar2=None, op0=ALU.mult)
+            nc.vector.tensor_scalar(out=negmean[m][:], in0=s1[:], scalar1=-1.0 / n, scalar2=None, op0=ALU.mult)
             d = small("d_%d" % m)
-            nc.vector.tensor_tensor(out=d[:], in0=mean[:], in1=shift[m][:], op=ALU.add)
+            nc.vector.tensor_tensor(out=d[:], in0=shift[m][:], in1=negmean[m][:], op=ALU.subtract)
             d2 = small("d2_%d" % m)
             nc.vector.scalar_tensor_tensor(out=d2[:], in0=d[:], scalar=n, in1=d[:], op0=ALU.mult, op1=ALU.mult)
             var = small("var_%d" % m)
@@ -179,26 +175,60 @@ def tile_layernormlstmcell_kernel(
             nc.gpsimd.tensor_tensor(out=std[:], in0=var[:], in1=half[:], op=ALU.pow)
             nc.vector.tensor_scalar(out=std[:], in0=std[:], scalar1=EPS, scalar2=None, op0=ALU.add)
             nc.vector.reciprocal(out=rinv[m][:], in_=std[:])
-            alpha = small("alpha_%d" % m)
-            nc.vector.scalar_tensor_tensor(out=alpha[:], in0=mean[:], scalar=-1.0, in1=rinv[m][:], op0=ALU.mult, op1=ALU.mult)
-            nc.vector.tensor_copy(out=cview[:, :, m, 0], in_=alpha[:])
-            rem = small("rem_%d" % m)
-            nc.vector.tensor_tensor(out=rem[:], in0=alpha[:], in1=cview[:, :, m, 0], op=ALU.subtract)
-            nc.vector.tensor_copy(out=cview[:, :, m, 1], in_=rem[:])
-            rem2 = small("rem2_%d" % m)
-            nc.vector.tensor_tensor(out=rem2[:], in0=rem[:], in1=cview[:, :, m, 1], op=ALU.subtract)
-            nc.vector.tensor_copy(out=cview[:, :, m, 2], in_=rem2[:])
+            nc.vector.tensor_tensor(out=nbias[m][:], in0=negmean[m][:], in1=rinv[m][:], op=ALU.mult)
+
+        def norm(m, gate, on_scalar):
+            cols = slice(gate * H, (gate + 1) * H)
+            for r in range(RT):
+                if r in on_scalar:
+                    nc.scalar.activation(
+                        out=va[m][:, r, cols], in_=va[m][:, r, cols], func=ACT.Identity,
+                        scale=rinv[m][:, r:r + 1], bias=nbias[m][:, r:r + 1],
+                    )
+                else:
+                    nc.vector.tensor_scalar(
+                        out=va[m][:, r, cols], in0=va[m][:, r, cols],
+                        scalar1=negmean[m][:, r:r + 1], scalar2=rinv[m][:, r:r + 1],
+                        op0=ALU.add, op1=ALU.mult,
+                    )
+
+        def fphase(q):
+            for jt in range(4 * q, 4 * q + 4):
+                cols = slice(jt * P, (jt + 1) * P)
+                banks = []
+                for m in range(2):
+                    pf = psum.tile([P, RT, P], F32, tag="tp", name="pf")
+                    for r in range(RT):
+                        nc.tensor.transpose(pf[:, r, :], va[m][:, r, cols], ident_f[:])
+                    banks.append(pf)
+                nc.scalar.activation(
+                    out=va[0][:, :, cols], in_=banks[0][:], func=ACT.Identity,
+                    scale=vcf[:, jt:jt + 1], bias=lbc[:, jt:jt + 1],
+                )
+                nc.vector.scalar_tensor_tensor(
+                    out=va[0][:, :, cols], in0=banks[1][:], scalar=vcf[:, 32 + jt:33 + jt], in1=va[0][:, :, cols],
+                    op0=ALU.mult, op1=ALU.add,
+                )
+
+        def bphase(q):
+            gate = q // 2
+            cols = slice(q * CH, (q + 1) * CH)
+            for r in range(RT):
+                pb = psum.tile([P, CH], F32, tag="acc", name="pb")
+                for t in range(4):
+                    jt = 4 * q + t
+                    nc.tensor.transpose(pb[:, t * P:(t + 1) * P], va[0][:, r, jt * P:(jt + 1) * P], ident_f[:])
+                if gate == 1:
+                    nc.scalar.activation(out=va[1][:, r, cols], in_=pb[:], func=ACT.Sigmoid, bias=negone[:, 0:1], scale=1.0)
+                elif gate == 3:
+                    nc.scalar.activation(out=va[1][:, r, cols], in_=pb[:], func=ACT.Tanh)
+                else:
+                    nc.scalar.activation(out=va[1][:, r, cols], in_=pb[:], func=ACT.Sigmoid)
 
         prep(acts[0], acodes[0], ascales[0])
         nxt = prep_w(0)
-        for m in range(2):
-            nc.sync.dma_start(out=krhs[3 * m:3 * m + 3, :], in_=ln_w[m].rearrange("o n -> (o n)").partition_broadcast(3))
-            nc.sync.dma_start(out=krhs[6 + m:7 + m, :], in_=ln_b[m])
-        nc.sync.dma_start(out=wbc[0][:], in_=ln_w[0].rearrange("o n -> (o n)").partition_broadcast(P))
         for idx in range(2 * NCH):
             cur = nxt
-            if idx == 3:
-                nc.sync.dma_start(out=wbc[1][:], in_=ln_w[1].rearrange("o n -> (o n)").partition_broadcast(P))
             if idx == NCH - 2:
                 prep(acts[1], acodes[1], ascales[1])
             if idx == NCH + 2:
@@ -210,12 +240,9 @@ def tile_layernormlstmcell_kernel(
             work(idx, cur)
             if idx == NCH:
                 stats(0)
+            if NCH + 1 <= idx <= NCH + 4:
+                norm(0, (1, 0, 3, 2)[idx - NCH - 1], ())
         stats(1)
-
-        ctp = psum.tile([P, RT * P], BF16, tag="tp", name="ctp")
-        for r in range(RT):
-            nc.tensor.transpose(ctp[:, r * P:(r + 1) * P], coef[:, r, :], ident_b[:])
-        nc.scalar.copy(out=coefT[:], in_=ctp[:])
 
         s3 = const.tile([P, RT], F32, name="s3")
         q3 = const.tile([P, RT], F32, name="q3")
@@ -223,48 +250,14 @@ def tile_layernormlstmcell_kernel(
         r3 = const.tile([P, RT], F32, name="r3")
 
         def parts(r):
-            x = v[0][r]
-            tmp = v[1][r]
-            return (x[:, 0:H], x[:, H:2 * H], x[:, 2 * H:3 * H], x[:, 3 * H:4 * H],
-                    tmp[:, 0:H], tmp[:, H:2 * H], tmp[:, 2 * H:3 * H], tmp[:, 3 * H:4 * H])
-
-        def zstep(r):
-            x = v[0][r]
-            for n in range(NCH):
-                cols = slice(n * CH, (n + 1) * CH)
-                kp = psum.tile([P, CH], F32, tag=("acc" if n % 2 == 0 else "tp"), name="kp")
-                nc.tensor.matmul(out=kp[:], lhsT=coefT[:, r * P:(r + 1) * P], rhs=krhs[:, cols], start=True, stop=True)
-                nc.vector.scalar_tensor_tensor(
-                    out=x[:, cols], in0=x[:, cols], scalar=rinv[0][:, r:r + 1], in1=kp[:],
-                    op0=ALU.mult, op1=ALU.add,
-                )
-
-        def xstep(r):
-            x = v[0][r]
-            tmp = v[1][r]
-            for gate in (1, 0, 3, 2):
-                cols = slice(gate * H, (gate + 1) * H)
-                nc.vector.scalar_tensor_tensor(
-                    out=x[:, cols], in0=tmp[:, cols], scalar=rinv[1][:, r:r + 1], in1=x[:, cols],
-                    op0=ALU.mult, op1=ALU.add,
-                )
-
-        def gates(r):
-            gi, gf, go, gc, t0, t1, cn, hn = parts(r)
-            nc.scalar.activation(out=gf, in_=gf, func=ACT.Sigmoid, bias=negone[:, 0:1], scale=1.0)
-            nc.scalar.activation(out=gi, in_=gi, func=ACT.Sigmoid)
-            nc.scalar.activation(out=gc, in_=gc, func=ACT.Tanh)
-            nc.scalar.activation(out=go, in_=go, func=ACT.Sigmoid)
-
-        def ab(r):
-            gi, gf, go, gc, t0, t1, cn, hn = parts(r)
-            eng = nc.vector
-            eng.tensor_tensor(out=t0, in0=gf, in1=cx_sb[:, r, :], op=ALU.mult)
-            eng.tensor_tensor(out=t1, in0=gi, in1=gc, op=ALU.mult)
+            return (va[1][:, r, 0:H], va[1][:, r, H:2 * H], va[1][:, r, 2 * H:3 * H], va[1][:, r, 3 * H:4 * H],
+                    va[0][:, r, 0:H], va[0][:, r, H:2 * H], va[0][:, r, 3 * H:4 * H], va[0][:, r, 2 * H:3 * H])
 
         def c3(r):
             gi, gf, go, gc, t0, t1, cn, hn = parts(r)
             rr = slice(r, r + 1)
+            nc.vector.tensor_tensor(out=t0, in0=gf, in1=cx_sb[:, r, :], op=ALU.mult)
+            nc.vector.tensor_tensor(out=t1, in0=gi, in1=gc, op=ALU.mult)
             nc.vector.scalar_tensor_tensor(out=cn, in0=t0, scalar=1.0, in1=t1, op0=ALU.mult, op1=ALU.add, accum_out=s3[:, rr])
             nc.sync.dma_start(out=out_1[r * P:(r + 1) * P, :], in_=cn)
             nc.vector.tensor_scalar(out=negm3[:, rr], in0=s3[:, rr], scalar1=-1.0 / H, scalar2=None, op0=ALU.mult)
@@ -288,12 +281,35 @@ def tile_layernormlstmcell_kernel(
             nc.vector.tensor_tensor(out=hn, in0=go, in1=t1, op=ALU.mult)
             nc.sync.dma_start(out=out_0[r * P:(r + 1) * P, :], in_=hn)
 
-        order = [
-            (zstep, 0), (zstep, 1), (xstep, 0), (gates, 0),
-            (zstep, 2), (xstep, 1), (ab, 0), (gates, 1), (c3, 0),
-            (zstep, 3), (xstep, 2), (ab, 1), (fin1, 0), (gates, 2), (c3, 1), (fin2, 0),
-            (xstep, 3), (ab, 2), (fin1, 1), (gates, 3), (c3, 2), (fin2, 1),
-            (ab, 3), (fin1, 2), (c3, 3), (fin2, 2), (fin1, 3), (fin2, 3),
-        ]
-        for step, r in order:
-            step(r)
+        norm(1, 1, (2, 3))
+        norm(1, 0, (2, 3))
+        fphase(2)
+        norm(1, 3, ())
+        fphase(0)
+        bphase(2)
+        fphase(6)
+        bphase(0)
+        norm(1, 2, ())
+        fphase(3)
+        bphase(6)
+        fphase(1)
+        bphase(3)
+        fphase(7)
+        bphase(1)
+        fphase(4)
+        bphase(7)
+        c3(0)
+        c3(1)
+        fphase(5)
+        bphase(4)
+        c3(2)
+        fin1(0)
+        c3(3)
+        bphase(5)
+        fin1(1)
+        fin2(0)
+        fin1(2)
+        fin2(1)
+        fin1(3)
+        fin2(2)
+        fin2(3)

@@ -63,21 +63,28 @@ def tile_layernormlstmcell_kernel(
         negmean = [const.tile([P, RT], F32, name="negmean%d" % m) for m in range(2)]
         nbias = [const.tile([P, RT], F32, name="nbias%d" % m) for m in range(2)]
 
+        vcf = const.tile([P, P], F32, name="vcf")
+        lbc = const.tile([P, 32], F32, name="lbc")
         vr = const.tile([P, P], BF16, name="vr")
         nc.scalar.dma_start(out=vr[0:32, :], in_=ln_i2h_w.rearrange("o (t j) -> (o t) j", j=P))
         nc.scalar.dma_start(out=vr[32:64, :], in_=ln_h2h_w.rearrange("o (t j) -> (o t) j", j=P))
         nc.scalar.dma_start(out=vr[64:96, :], in_=ln_i2h_b.rearrange("o (t j) -> (o t) j", j=P))
         nc.scalar.dma_start(out=vr[96:128, :], in_=ln_h2h_b.rearrange("o (t j) -> (o t) j", j=P))
-        vps = psum.tile([P, P], BF16, tag="tp", name="vps")
-        nc.tensor.transpose(vps[:], vr[:], ident_b[:])
-        vcf = const.tile([P, P], F32, name="vcf")
-        nc.vector.tensor_copy(out=vcf[:], in_=vps[:])
-        lbc = const.tile([P, 32], F32, name="lbc")
-        nc.vector.tensor_tensor(out=lbc[:], in0=vcf[:, 64:96], in1=vcf[:, 96:128], op=ALU.add)
 
-        def prep(rows, codes, scales):
+        def vecs():
+            vps = psum.tile([P, P], BF16, tag="tp", name="vps")
+            nc.tensor.transpose(vps[:], vr[:], ident_b[:])
+            nc.vector.tensor_copy(out=vcf[:], in_=vps[:])
+            nc.vector.tensor_tensor(out=lbc[:], in0=vcf[:, 64:96], in1=vcf[:, 96:128], op=ALU.add)
+
+        def prep(rows, codes, scales, pieces=1):
             raw = stage.tile([P, 4, K], BF16, tag="raw", bufs=3, name="raw")
-            nc.sync.dma_start(out=raw[:], in_=rows.rearrange("(t p) k -> p t k", p=P))
+            step = 4 // pieces
+            for t in range(0, 4, step):
+                nc.sync.dma_start(
+                    out=raw[:, t:t + step, :],
+                    in_=rows[t * P:(t + step) * P, :].rearrange("(t p) k -> p t k", p=P),
+                )
             grouped = stage.tile([P, 2048], F32, tag="grouped", name="grouped", align_bytes=64)
             gview = grouped[:].rearrange("p (g j u) -> p g j u", g=2, u=2)
             for g in range(2):
@@ -112,7 +119,7 @@ def tile_layernormlstmcell_kernel(
             m, c = divmod(idx, NCH)
             wcodes = stage.tile([P, 1024], U32, tag="wcodes", name="wcodes", align_bytes=64)
             wscales = stage.tile([P, 1024], U8, tag="wscales", name="wscales", align_bytes=64)
-            prep(weights[m][c * CH:(c + 1) * CH, :], wcodes, wscales)
+            prep(weights[m][c * CH:(c + 1) * CH, :], wcodes, wscales, pieces=(2 if idx == 0 else 1))
             bbc = stage.tile([P, CH], BF16, tag="bbc", bufs=3, name="bbc")
             nc.sync.dma_start(out=bbc[:], in_=biases[m][c * CH:(c + 1) * CH].partition_broadcast(P))
             return wcodes, wscales, bbc
@@ -192,21 +199,25 @@ def tile_layernormlstmcell_kernel(
                         op0=ALU.add, op1=ALU.mult,
                     )
 
-        def fphase(q):
+        def fa(q):
             for jt in range(4 * q, 4 * q + 4):
                 cols = slice(jt * P, (jt + 1) * P)
-                banks = []
-                for m in range(2):
-                    pf = psum.tile([P, RT, P], F32, tag="tp", name="pf")
-                    for r in range(RT):
-                        nc.tensor.transpose(pf[:, r, :], va[m][:, r, cols], ident_f[:])
-                    banks.append(pf)
+                pf = psum.tile([P, RT, P], F32, tag="tp", name="pf")
+                for r in range(RT):
+                    nc.tensor.transpose(pf[:, r, :], va[0][:, r, cols], ident_f[:])
                 nc.scalar.activation(
-                    out=va[0][:, :, cols], in_=banks[0][:], func=ACT.Identity,
+                    out=va[0][:, :, cols], in_=pf[:], func=ACT.Identity,
                     scale=vcf[:, jt:jt + 1], bias=lbc[:, jt:jt + 1],
                 )
+
+        def fb(q):
+            for jt in range(4 * q, 4 * q + 4):
+                cols = slice(jt * P, (jt + 1) * P)
+                pf = psum.tile([P, RT, P], F32, tag="tp", name="pf")
+                for r in range(RT):
+                    nc.tensor.transpose(pf[:, r, :], va[1][:, r, cols], ident_f[:])
                 nc.vector.scalar_tensor_tensor(
-                    out=va[0][:, :, cols], in0=banks[1][:], scalar=vcf[:, 32 + jt:33 + jt], in1=va[0][:, :, cols],
+                    out=va[0][:, :, cols], in0=pf[:], scalar=vcf[:, 32 + jt:33 + jt], in1=va[0][:, :, cols],
                     op0=ALU.mult, op1=ALU.add,
                 )
 
@@ -225,7 +236,7 @@ def tile_layernormlstmcell_kernel(
                 else:
                     nc.scalar.activation(out=va[1][:, r, cols], in_=pb[:], func=ACT.Sigmoid)
 
-        prep(acts[0], acodes[0], ascales[0])
+        prep(acts[0], acodes[0], ascales[0], pieces=4)
         nxt = prep_w(0)
         for idx in range(2 * NCH):
             cur = nxt
@@ -240,9 +251,15 @@ def tile_layernormlstmcell_kernel(
             work(idx, cur)
             if idx == NCH:
                 stats(0)
-            if NCH + 1 <= idx <= NCH + 4:
-                norm(0, (1, 0, 3, 2)[idx - NCH - 1], ())
+            if idx == 2:
+                vecs()
+            if idx in (NCH + 2, NCH + 4):
+                norm(0, (1, 0)[(idx - NCH - 2) // 2], (3,))
+        fa(2)
+        fa(0)
         stats(1)
+        norm(0, 3, ())
+        norm(0, 2, ())
 
         s3 = const.tile([P, RT], F32, name="s3")
         q3 = const.tile([P, RT], F32, name="q3")
@@ -253,13 +270,24 @@ def tile_layernormlstmcell_kernel(
             return (va[1][:, r, 0:H], va[1][:, r, H:2 * H], va[1][:, r, 2 * H:3 * H], va[1][:, r, 3 * H:4 * H],
                     va[0][:, r, 0:H], va[0][:, r, H:2 * H], va[0][:, r, 3 * H:4 * H], va[0][:, r, 2 * H:3 * H])
 
+        s3h = const.tile([P, RT, 2], F32, name="s3h")
+
+        def cab(hf):
+            cc = slice(hf * CH, (hf + 1) * CH)
+            for r in range(RT):
+                gi, gf, go, gc, t0, t1, cn, hn = parts(r)
+                nc.vector.tensor_tensor(out=t0[:, cc], in0=gf[:, cc], in1=cx_sb[:, r, cc], op=ALU.mult)
+                nc.vector.tensor_tensor(out=t1[:, cc], in0=gi[:, cc], in1=gc[:, cc], op=ALU.mult)
+                nc.vector.scalar_tensor_tensor(
+                    out=cn[:, cc], in0=t0[:, cc], scalar=1.0, in1=t1[:, cc], op0=ALU.mult, op1=ALU.add,
+                    accum_out=s3h[:, r, hf:hf + 1],
+                )
+
         def c3(r):
             gi, gf, go, gc, t0, t1, cn, hn = parts(r)
             rr = slice(r, r + 1)
-            nc.vector.tensor_tensor(out=t0, in0=gf, in1=cx_sb[:, r, :], op=ALU.mult)
-            nc.vector.tensor_tensor(out=t1, in0=gi, in1=gc, op=ALU.mult)
-            nc.vector.scalar_tensor_tensor(out=cn, in0=t0, scalar=1.0, in1=t1, op0=ALU.mult, op1=ALU.add, accum_out=s3[:, rr])
             nc.sync.dma_start(out=out_1[r * P:(r + 1) * P, :], in_=cn)
+            nc.vector.tensor_tensor(out=s3[:, rr], in0=s3h[:, r, 0:1], in1=s3h[:, r, 1:2], op=ALU.add)
             nc.vector.tensor_scalar(out=negm3[:, rr], in0=s3[:, rr], scalar1=-1.0 / H, scalar2=None, op0=ALU.mult)
             nc.scalar.activation(out=t0, in_=cn, func=ACT.Square, bias=negm3[:, rr], scale=1.0, accum_out=q3[:, rr])
             nc.vector.scalar_tensor_tensor(out=t1, in0=cn, scalar=negm3[:, rr], in1=w3bc[:], op0=ALU.add, op1=ALU.mult)
@@ -283,24 +311,32 @@ def tile_layernormlstmcell_kernel(
 
         norm(1, 1, (2, 3))
         norm(1, 0, (2, 3))
-        fphase(2)
-        norm(1, 3, ())
-        fphase(0)
+        fb(2)
+        norm(1, 3, (3,))
+        fa(6)
+        fb(0)
         bphase(2)
-        fphase(6)
+        fb(6)
         bphase(0)
-        norm(1, 2, ())
-        fphase(3)
+        fa(3)
+        norm(1, 2, (3,))
+        fb(3)
         bphase(6)
-        fphase(1)
+        fa(1)
+        cab(0)
+        fb(1)
         bphase(3)
-        fphase(7)
+        fa(7)
+        fb(7)
         bphase(1)
-        fphase(4)
+        fa(4)
+        fb(4)
         bphase(7)
+        fa(5)
+        cab(1)
+        fb(5)
         c3(0)
         c3(1)
-        fphase(5)
         bphase(4)
         c3(2)
         fin1(0)

@@ -77,7 +77,7 @@ def tile_layernormlstmcell_kernel(
             nc.vector.tensor_copy(out=vcf[:], in_=vps[:])
             nc.vector.tensor_tensor(out=lbc[:], in0=vcf[:, 64:96], in1=vcf[:, 96:128], op=ALU.add)
 
-        def prep(rows, codes, scales, pieces=1):
+        def prep_load(rows, pieces=1):
             raw = stage.tile([P, 4, K], BF16, tag="raw", bufs=3, name="raw")
             step = 4 // pieces
             for t in range(0, 4, step):
@@ -86,49 +86,56 @@ def tile_layernormlstmcell_kernel(
                     in_=rows[t * P:(t + step) * P, :].rearrange("(t p) k -> p t k", p=P),
                 )
             grouped = stage.tile([P, 2048], F32, tag="grouped", name="grouped", align_bytes=64)
-            gview = grouped[:].rearrange("p (g j u) -> p g j u", g=2, u=2)
-            for g in range(2):
-                for hf in range(2):
-                    tp = psum.tile([P, 2, 256], F32, tag="tp", name="tp")
-                    for u in range(2):
-                        for tt in range(2):
-                            q = 2 * g + u
-                            nc.tensor.transpose(
-                                tp[:, u, tt * P:(tt + 1) * P],
-                                raw[:, 2 * hf + tt, :].bitcast(F32)[:, q * P:(q + 1) * P],
-                                ident_f[:],
-                            )
-                    if g == 1 and hf == 1:
-                        nc.vector.tensor_copy(
-                            out=gview[:, g, hf * 256:(hf + 1) * 256, :],
-                            in_=tp[:].rearrange("p u j -> p j u"),
-                        )
-                    else:
-                        nc.scalar.copy(
-                            out=gview[:, g, hf * 256:(hf + 1) * 256, :],
-                            in_=tp[:].rearrange("p u j -> p j u"),
-                        )
-            for g in range(2):
-                nc.vector.quantize_mx(
-                    out=codes[:, g * 512:(g + 1) * 512].bitcast(FP8X4),
-                    scales=scales[:, g * 512:(g + 1) * 512],
-                    in_=grouped[:, g * 1024:(g + 1) * 1024].bitcast(BF16),
-                )
+            return raw, grouped
 
-        def prep_w(idx):
+        def prep_half(loaded, codes, scales, g):
+            raw, grouped = loaded
+            gview = grouped[:].rearrange("p (g j u) -> p g j u", g=2, u=2)
+            for hf in range(2):
+                tp = psum.tile([P, 2, 256], F32, tag="tp", name="tp")
+                for u in range(2):
+                    for tt in range(2):
+                        q = 2 * g + u
+                        nc.tensor.transpose(
+                            tp[:, u, tt * P:(tt + 1) * P],
+                            raw[:, 2 * hf + tt, :].bitcast(F32)[:, q * P:(q + 1) * P],
+                            ident_f[:],
+                        )
+                if g == 1 and hf == 1:
+                    nc.vector.tensor_copy(
+                        out=gview[:, g, hf * 256:(hf + 1) * 256, :],
+                        in_=tp[:].rearrange("p u j -> p j u"),
+                    )
+                else:
+                    nc.scalar.copy(
+                        out=gview[:, g, hf * 256:(hf + 1) * 256, :],
+                        in_=tp[:].rearrange("p u j -> p j u"),
+                    )
+            nc.vector.quantize_mx(
+                out=codes[:, g * 512:(g + 1) * 512].bitcast(FP8X4),
+                scales=scales[:, g * 512:(g + 1) * 512],
+                in_=grouped[:, g * 1024:(g + 1) * 1024].bitcast(BF16),
+            )
+
+        def prep(rows, codes, scales, pieces=1):
+            loaded = prep_load(rows, pieces)
+            prep_half(loaded, codes, scales, 0)
+            prep_half(loaded, codes, scales, 1)
+
+        def load_w(idx):
             m, c = divmod(idx, NCH)
             wcodes = stage.tile([P, 1024], U32, tag="wcodes", name="wcodes", align_bytes=64)
             wscales = stage.tile([P, 1024], U8, tag="wscales", name="wscales", align_bytes=64)
-            prep(weights[m][c * CH:(c + 1) * CH, :], wcodes, wscales, pieces=(2 if idx == 0 else 1))
+            loaded = prep_load(weights[m][c * CH:(c + 1) * CH, :], pieces=(2 if idx == 0 else 1))
             bbc = stage.tile([P, CH], BF16, tag="bbc", bufs=3, name="bbc")
             nc.sync.dma_start(out=bbc[:], in_=biases[m][c * CH:(c + 1) * CH].partition_broadcast(P))
-            return wcodes, wscales, bbc
+            return loaded, (wcodes, wscales, bbc)
 
-        def work(idx, ops):
+        def mx_rows(idx, ops, row_tiles):
             m, c = divmod(idx, NCH)
             wcodes, wscales, bbc = ops
             cols = slice(c * CH, (c + 1) * CH)
-            for r in range(RT):
+            for r in row_tiles:
                 acc = psum.tile([P, CH], F32, tag="acc", name="acc")
                 for g in range(2):
                     a_cols = slice(g * B + r * P, g * B + (r + 1) * P)
@@ -147,6 +154,10 @@ def tile_layernormlstmcell_kernel(
                     out=va[m][:, r, cols], in0=acc[:], scalar=1.0, in1=bbc[:],
                     op0=ALU.mult, op1=ALU.add, accum_out=sums[:, k:k + 1],
                 )
+
+        def squares(idx):
+            m, c = divmod(idx, NCH)
+            cols = slice(c * CH, (c + 1) * CH)
             if c == 0:
                 first = sums[:, m * RT * NCH:(m + 1) * RT * NCH].rearrange("p (r c) -> p r c", c=NCH)[:, :, 0]
                 nc.vector.tensor_scalar(
@@ -163,7 +174,9 @@ def tile_layernormlstmcell_kernel(
         def small(name):
             return const.tile([P, RT], F32, name=name)
 
-        def stats(m):
+        stat_std = [small("std_%d" % m) for m in range(2)]
+
+        def stats_a(m):
             n = float(G4)
             seg = slice(m * RT * NCH, (m + 1) * RT * NCH)
             s1 = small("s1_%d" % m)
@@ -178,8 +191,10 @@ def tile_layernormlstmcell_kernel(
             var = small("var_%d" % m)
             nc.vector.tensor_tensor(out=var[:], in0=q1[:], in1=d2[:], op=ALU.subtract)
             nc.vector.tensor_scalar(out=var[:], in0=var[:], scalar1=1.0 / (n - 1.0), scalar2=0.0, op0=ALU.mult, op1=ALU.max)
-            std = small("std_%d" % m)
-            nc.gpsimd.tensor_tensor(out=std[:], in0=var[:], in1=half[:], op=ALU.pow)
+            nc.gpsimd.tensor_tensor(out=stat_std[m][:], in0=var[:], in1=half[:], op=ALU.pow)
+
+        def stats_b(m):
+            std = stat_std[m]
             nc.vector.tensor_scalar(out=std[:], in0=std[:], scalar1=EPS, scalar2=None, op0=ALU.add)
             nc.vector.reciprocal(out=rinv[m][:], in_=std[:])
             nc.vector.tensor_tensor(out=nbias[m][:], in0=negmean[m][:], in1=rinv[m][:], op=ALU.mult)
@@ -237,7 +252,9 @@ def tile_layernormlstmcell_kernel(
                     nc.scalar.activation(out=va[1][:, r, cols], in_=pb[:], func=ACT.Sigmoid)
 
         prep(acts[0], acodes[0], ascales[0], pieces=4)
-        nxt = prep_w(0)
+        loaded, nxt = load_w(0)
+        prep_half(loaded, nxt[0], nxt[1], 0)
+        prep_half(loaded, nxt[0], nxt[1], 1)
         for idx in range(2 * NCH):
             cur = nxt
             if idx == NCH - 2:
@@ -246,20 +263,29 @@ def tile_layernormlstmcell_kernel(
                 nc.sync.dma_start(out=cx_sb[:], in_=cx.rearrange("(r p) h -> p r h", p=P))
                 nc.sync.dma_start(out=w3bc[:], in_=ln_h2o_w.rearrange("o n -> (o n)").partition_broadcast(P))
                 nc.sync.dma_start(out=b3bc[:], in_=ln_h2o_b.rearrange("o n -> (o n)").partition_broadcast(P))
-            if idx + 1 < 2 * NCH:
-                nxt = prep_w(idx + 1)
-            work(idx, cur)
+            more = idx + 1 < 2 * NCH
+            if more:
+                loaded, nxt = load_w(idx + 1)
+                prep_half(loaded, nxt[0], nxt[1], 0)
+            mx_rows(idx, cur, (0, 1))
+            if more:
+                prep_half(loaded, nxt[0], nxt[1], 1)
+            mx_rows(idx, cur, (2, 3))
+            squares(idx)
             if idx == NCH:
-                stats(0)
+                stats_a(0)
+            if idx == NCH + 1:
+                stats_b(0)
             if idx == 2:
                 vecs()
             if idx in (NCH + 2, NCH + 4):
                 norm(0, (1, 0)[(idx - NCH - 2) // 2], (3,))
         fa(2)
         fa(0)
-        stats(1)
-        norm(0, 3, ())
-        norm(0, 2, ())
+        stats_a(1)
+        norm(0, 3, (3,))
+        fa(6)
+        stats_b(1)
 
         s3 = const.tile([P, RT], F32, name="s3")
         q3 = const.tile([P, RT], F32, name="q3")
@@ -292,13 +318,19 @@ def tile_layernormlstmcell_kernel(
             nc.scalar.activation(out=t0, in_=cn, func=ACT.Square, bias=negm3[:, rr], scale=1.0, accum_out=q3[:, rr])
             nc.vector.scalar_tensor_tensor(out=t1, in0=cn, scalar=negm3[:, rr], in1=w3bc[:], op0=ALU.add, op1=ALU.mult)
 
-        def fin1(r):
+        var3s = [const.tile([P, 1], F32, name="var3_%d" % r) for r in range(RT)]
+        std3s = [const.tile([P, 1], F32, name="std3_%d" % r) for r in range(RT)]
+
+        def fin1a(r):
+            rr = slice(r, r + 1)
+            nc.vector.tensor_scalar(out=var3s[r][:], in0=q3[:, rr], scalar1=1.0 / (H - 1.0), scalar2=None, op0=ALU.mult)
+            nc.gpsimd.tensor_tensor(out=std3s[r][:], in0=var3s[r][:], in1=half[:, 0:1], op=ALU.pow)
+
+        def fin1b(r):
             gi, gf, go, gc, t0, t1, cn, hn = parts(r)
             rr = slice(r, r + 1)
-            var3 = const.tile([P, 1], F32, name="var3_%d" % r)
-            std3 = const.tile([P, 1], F32, name="std3_%d" % r)
-            nc.vector.tensor_scalar(out=var3[:], in0=q3[:, rr], scalar1=1.0 / (H - 1.0), scalar2=None, op0=ALU.mult)
-            nc.gpsimd.tensor_tensor(out=std3[:], in0=var3[:], in1=half[:, 0:1], op=ALU.pow)
+            var3 = var3s[r]
+            std3 = std3s[r]
             nc.vector.tensor_scalar(out=var3[:], in0=std3[:], scalar1=EPS, scalar2=None, op0=ALU.add)
             nc.vector.reciprocal(out=r3[:, rr], in_=var3[:])
             nc.vector.scalar_tensor_tensor(out=t1, in0=t1, scalar=r3[:, rr], in1=b3bc[:], op0=ALU.mult, op1=ALU.add)
@@ -312,40 +344,44 @@ def tile_layernormlstmcell_kernel(
         norm(1, 1, (2, 3))
         norm(1, 0, (2, 3))
         fb(2)
-        norm(1, 3, (3,))
-        fa(6)
+        norm(1, 3, (2, 3))
         fb(0)
         bphase(2)
         fb(6)
         bphase(0)
+        norm(0, 2, (3,))
         fa(3)
-        norm(1, 2, (3,))
         fb(3)
         bphase(6)
-        fa(1)
         cab(0)
+        fa(1)
         fb(1)
         bphase(3)
+        norm(1, 2, (3,))
         fa(7)
         fb(7)
         bphase(1)
         fa(4)
         fb(4)
         bphase(7)
-        fa(5)
         cab(1)
+        fa(5)
         fb(5)
         c3(0)
         c3(1)
+        fin1a(0)
         bphase(4)
         c3(2)
-        fin1(0)
+        fin1a(1)
+        fin1b(0)
         c3(3)
+        fin1a(2)
+        fin1b(1)
         bphase(5)
-        fin1(1)
         fin2(0)
-        fin1(2)
+        fin1a(3)
+        fin1b(2)
         fin2(1)
-        fin1(3)
+        fin1b(3)
         fin2(2)
         fin2(3)

@@ -155,14 +155,17 @@ def tile_layernormlstmcell_kernel(
                     op0=ALU.mult, op1=ALU.add, accum_out=sums[:, k:k + 1],
                 )
 
-        def squares(idx):
+        def first_shift(idx):
             m, c = divmod(idx, NCH)
-            cols = slice(c * CH, (c + 1) * CH)
             if c == 0:
                 first = sums[:, m * RT * NCH:(m + 1) * RT * NCH].rearrange("p (r c) -> p r c", c=NCH)[:, :, 0]
                 nc.vector.tensor_scalar(
                     out=shift[m][:], in0=first, scalar1=-1.0 / CH, scalar2=None, op0=ALU.mult,
                 )
+
+        def squares(idx):
+            m, c = divmod(idx, NCH)
+            cols = slice(c * CH, (c + 1) * CH)
             for r in range(RT):
                 k = (m * RT + r) * NCH + c
                 junk = stage.tile([P, CH], BF16, tag="junk", name="junk")
@@ -251,35 +254,36 @@ def tile_layernormlstmcell_kernel(
                 else:
                     nc.scalar.activation(out=va[1][:, r, cols], in_=pb[:], func=ACT.Sigmoid)
 
-        prep(acts[0], acodes[0], ascales[0], pieces=4)
-        loaded, nxt = load_w(0)
-        prep_half(loaded, nxt[0], nxt[1], 0)
-        prep_half(loaded, nxt[0], nxt[1], 1)
-        for idx in range(2 * NCH):
-            cur = nxt
-            if idx == NCH - 2:
-                prep(acts[1], acodes[1], ascales[1])
-            if idx == NCH + 2:
-                nc.sync.dma_start(out=cx_sb[:], in_=cx.rearrange("(r p) h -> p r h", p=P))
-                nc.sync.dma_start(out=w3bc[:], in_=ln_h2o_w.rearrange("o n -> (o n)").partition_broadcast(P))
-                nc.sync.dma_start(out=b3bc[:], in_=ln_h2o_b.rearrange("o n -> (o n)").partition_broadcast(P))
-            more = idx + 1 < 2 * NCH
-            if more:
-                loaded, nxt = load_w(idx + 1)
-                prep_half(loaded, nxt[0], nxt[1], 0)
-            mx_rows(idx, cur, (0, 1))
-            if more:
-                prep_half(loaded, nxt[0], nxt[1], 1)
-            mx_rows(idx, cur, (2, 3))
-            squares(idx)
-            if idx == NCH:
-                stats_a(0)
-            if idx == NCH + 1:
-                stats_b(0)
-            if idx == 2:
-                vecs()
-            if idx in (NCH + 2, NCH + 4):
-                norm(0, (1, 0)[(idx - NCH - 2) // 2], (3,))
+        with tc.manual_schedule():
+            prep(acts[0], acodes[0], ascales[0], pieces=4)
+            loaded, nxt = load_w(0)
+            prep_half(loaded, nxt[0], nxt[1], 0)
+            prep_half(loaded, nxt[0], nxt[1], 1)
+            for idx in range(2 * NCH):
+                cur = nxt
+                if idx == NCH - 2:
+                    prep(acts[1], acodes[1], ascales[1])
+                if idx == NCH + 2:
+                    nc.sync.dma_start(out=cx_sb[:], in_=cx.rearrange("(r p) h -> p r h", p=P))
+                    nc.sync.dma_start(out=w3bc[:], in_=ln_h2o_w.rearrange("o n -> (o n)").partition_broadcast(P))
+                    nc.sync.dma_start(out=b3bc[:], in_=ln_h2o_b.rearrange("o n -> (o n)").partition_broadcast(P))
+                if idx + 1 < 2 * NCH:
+                    loaded, nxt = load_w(idx + 1)
+                    prep_half(loaded, nxt[0], nxt[1], 0)
+                    prep_half(loaded, nxt[0], nxt[1], 1)
+                if idx >= 1:
+                    squares(idx - 1)
+                mx_rows(idx, cur, (0, 1, 2, 3))
+                first_shift(idx)
+                if idx == 2:
+                    vecs()
+                if idx == NCH + 1:
+                    stats_a(0)
+                if idx == NCH + 2:
+                    stats_b(0)
+                if idx in (NCH + 3, NCH + 5):
+                    norm(0, (1, 0)[(idx - NCH - 3) // 2], (3,))
+            squares(2 * NCH - 1)
         fa(2)
         fa(0)
         stats_a(1)

@@ -88,7 +88,7 @@ def tile_layernormlstmcell_kernel(
             grouped = stage.tile([P, 2048], F32, tag="grouped", name="grouped", align_bytes=64)
             return raw, grouped
 
-        def prep_half(loaded, codes, scales, g):
+        def turn(loaded, g, vector_hf):
             raw, grouped = loaded
             gview = grouped[:].rearrange("p (g j u) -> p g j u", g=2, u=2)
             for hf in range(2):
@@ -101,7 +101,7 @@ def tile_layernormlstmcell_kernel(
                             raw[:, 2 * hf + tt, :].bitcast(F32)[:, q * P:(q + 1) * P],
                             ident_f[:],
                         )
-                if g == 1 and hf == 1:
+                if hf == vector_hf:
                     nc.vector.tensor_copy(
                         out=gview[:, g, hf * 256:(hf + 1) * 256, :],
                         in_=tp[:].rearrange("p u j -> p j u"),
@@ -111,6 +111,9 @@ def tile_layernormlstmcell_kernel(
                         out=gview[:, g, hf * 256:(hf + 1) * 256, :],
                         in_=tp[:].rearrange("p u j -> p j u"),
                     )
+
+        def quant(loaded, codes, scales, g):
+            raw, grouped = loaded
             nc.vector.quantize_mx(
                 out=codes[:, g * 512:(g + 1) * 512].bitcast(FP8X4),
                 scales=scales[:, g * 512:(g + 1) * 512],
@@ -119,8 +122,10 @@ def tile_layernormlstmcell_kernel(
 
         def prep(rows, codes, scales, pieces=1):
             loaded = prep_load(rows, pieces)
-            prep_half(loaded, codes, scales, 0)
-            prep_half(loaded, codes, scales, 1)
+            turn(loaded, 0, 1)
+            turn(loaded, 1, 2)
+            quant(loaded, codes, scales, 0)
+            quant(loaded, codes, scales, 1)
 
         def load_w(idx):
             m, c = divmod(idx, NCH)
@@ -163,10 +168,10 @@ def tile_layernormlstmcell_kernel(
                     out=shift[m][:], in0=first, scalar1=-1.0 / CH, scalar2=None, op0=ALU.mult,
                 )
 
-        def squares(idx):
+        def squares(idx, row_tiles):
             m, c = divmod(idx, NCH)
             cols = slice(c * CH, (c + 1) * CH)
-            for r in range(RT):
+            for r in row_tiles:
                 k = (m * RT + r) * NCH + c
                 junk = stage.tile([P, CH], BF16, tag="junk", name="junk")
                 nc.scalar.activation(
@@ -257,8 +262,10 @@ def tile_layernormlstmcell_kernel(
         with tc.manual_schedule():
             prep(acts[0], acodes[0], ascales[0], pieces=4)
             loaded, nxt = load_w(0)
-            prep_half(loaded, nxt[0], nxt[1], 0)
-            prep_half(loaded, nxt[0], nxt[1], 1)
+            turn(loaded, 0, 1)
+            turn(loaded, 1, 2)
+            quant(loaded, nxt[0], nxt[1], 0)
+            quant(loaded, nxt[0], nxt[1], 1)
             for idx in range(2 * NCH):
                 cur = nxt
                 if idx == NCH - 2:
@@ -267,13 +274,21 @@ def tile_layernormlstmcell_kernel(
                     nc.sync.dma_start(out=cx_sb[:], in_=cx.rearrange("(r p) h -> p r h", p=P))
                     nc.sync.dma_start(out=w3bc[:], in_=ln_h2o_w.rearrange("o n -> (o n)").partition_broadcast(P))
                     nc.sync.dma_start(out=b3bc[:], in_=ln_h2o_b.rearrange("o n -> (o n)").partition_broadcast(P))
-                if idx + 1 < 2 * NCH:
+                more = idx + 1 < 2 * NCH
+                if more:
                     loaded, nxt = load_w(idx + 1)
-                    prep_half(loaded, nxt[0], nxt[1], 0)
-                    prep_half(loaded, nxt[0], nxt[1], 1)
+                    turn(loaded, 0, 1)
                 if idx >= 1:
-                    squares(idx - 1)
-                mx_rows(idx, cur, (0, 1, 2, 3))
+                    squares(idx - 1, (0, 1))
+                mx_rows(idx, cur, (0, 1))
+                if more:
+                    quant(loaded, nxt[0], nxt[1], 0)
+                    turn(loaded, 1, 2)
+                if idx >= 1:
+                    squares(idx - 1, (2, 3))
+                mx_rows(idx, cur, (2, 3))
+                if more:
+                    quant(loaded, nxt[0], nxt[1], 1)
                 first_shift(idx)
                 if idx == 2:
                     vecs()
@@ -283,7 +298,7 @@ def tile_layernormlstmcell_kernel(
                     stats_b(0)
                 if idx in (NCH + 3, NCH + 5):
                     norm(0, (1, 0)[(idx - NCH - 3) // 2], (3,))
-            squares(2 * NCH - 1)
+            squares(2 * NCH - 1, (0, 1, 2, 3))
         fa(2)
         fa(0)
         stats_a(1)

from contextlib import ExitStack

import concourse.masks as masks
import concourse.mybir as mybir

F32 = mybir.dt.float32
BF16 = mybir.dt.bfloat16
U32 = mybir.dt.uint32
U8 = mybir.dt.uint8
FP8X4 = mybir.dt.float8_e4m3fn_x4
ALU = mybir.AluOpType
ACT = mybir.ActivationFunctionType
AX = mybir.AxisListType

P = 128
B = 512
K = 1024
H = 1024
G4 = 4 * H
RT = B // P
CH = 512
NCH = G4 // CH
EPS = 1e-5

FLOPS = 2 * 2 * B * K * G4


def tile_layernormlstmcell_kernel(
    tc, inputs, hx, cx, w_i2h, b_i2h, w_h2h, b_h2h,
    ln_i2h_w, ln_i2h_b, ln_h2h_w, ln_h2h_b, ln_h2o_w, ln_h2o_b, out_0, out_1,
):
    nc = tc.nc
    acts = [inputs, hx]
    weights = [w_i2h, w_h2h]
    biases = [b_i2h, b_h2h]

    with ExitStack() as ctx:
        const = ctx.enter_context(tc.tile_pool(name="const", bufs=1))
        stage = ctx.enter_context(tc.tile_pool(name="stage", bufs=2))
        psum = ctx.enter_context(tc.psum_pool(name="psum", bufs=4))

        ident_f = const.tile([P, P], F32, name="ident_f")
        masks.make_identity(nc, ident_f[:])
        ident_b = const.tile([P, P], BF16, name="ident_b")
        masks.make_identity(nc, ident_b[:])

        half = const.tile([P, RT], F32, name="half")
        nc.vector.memset(half[:], 0.5)
        negone = const.tile([P, 1], F32, name="negone")
        nc.vector.memset(negone[:], -1.0)

        acodes = [const.tile([P, 2 * B], U32, name="acodes%d" % m, align_bytes=64) for m in range(2)]
        ascales = [const.tile([P, 2 * B], U8, name="ascales%d" % m, align_bytes=64) for m in range(2)]
        va = [const.tile([P, RT, G4], F32, name="va%d" % m) for m in range(2)]
        w3bc = const.tile([P, H], BF16, name="w3bc")
        b3bc = const.tile([P, H], BF16, name="b3bc")
        cx_sb = const.tile([P, RT, H], BF16, name="cx_sb")

        sums = const.tile([P, 2 * RT * NCH], F32, name="sums")
        sqs = const.tile([P, 2 * RT * NCH], F32, name="sqs")
        shift = [const.tile([P, RT], F32, name="shift%d" % m) for m in range(2)]
        rinv = [const.tile([P, RT], F32, name="rinv%d" % m) for m in range(2)]
        negmean = [const.tile([P, RT], F32, name="negmean%d" % m) for m in range(2)]
        nbias = [const.tile([P, RT], F32, name="nbias%d" % m) for m in range(2)]

        vcf = const.tile([P, P], F32, name="vcf")
        lbc = const.tile([P, 32], F32, name="lbc")
        vr = const.tile([P, P], BF16, name="vr")
        nc.scalar.dma_start(out=vr[0:32, :], in_=ln_i2h_w.rearrange("o (t j) -> (o t) j", j=P))
        nc.scalar.dma_start(out=vr[32:64, :], in_=ln_h2h_w.rearrange("o (t j) -> (o t) j", j=P))
        nc.scalar.dma_start(out=vr[64:96, :], in_=ln_i2h_b.rearrange("o (t j) -> (o t) j", j=P))
        nc.scalar.dma_start(out=vr[96:128, :], in_=ln_h2h_b.rearrange("o (t j) -> (o t) j", j=P))

        def vecs():
            vps = psum.tile([P, P], BF16, tag="tp", name="vps")
            nc.tensor.transpose(vps[:], vr[:], ident_b[:])
            nc.vector.tensor_copy(out=vcf[:], in_=vps[:])
            nc.vector.tensor_tensor(out=lbc[:], in0=vcf[:, 64:96], in1=vcf[:, 96:128], op=ALU.add)

        def prep_load(rows, pieces=1):
            raw = stage.tile([P, 4, K], BF16, tag="raw", bufs=3, name="raw")
            step = 4 // pieces
            for t in range(0, 4, step):
                nc.sync.dma_start(
                    out=raw[:, t:t + step, :],
                    in_=rows[t * P:(t + step) * P, :].rearrange("(t p) k -> p t k", p=P),
                )
            grouped = stage.tile([P, 2048], F32, tag="grouped", name="grouped", align_bytes=64)
            return raw, grouped

        def turn(loaded, g, vector_hf):
            raw, grouped = loaded
            gview = grouped[:].rearrange("p (g j u) -> p g j u", g=2, u=2)
            for hf in range(2):
                tp = psum.tile([P, 2, 256], F32, tag="tp", name="tp")
                for u in range(2):
                    for tt in range(2):
                        q = 2 * g + u
                        nc.tensor.transpose(
                            tp[:, u, tt * P:(tt + 1) * P],
                            raw[:, 2 * hf + tt, :].bitcast(F32)[:, q * P:(q + 1) * P],
                            ident_f[:],
                        )
                if hf == vector_hf:
                    nc.vector.tensor_copy(
                        out=gview[:, g, hf * 256:(hf + 1) * 256, :],
                        in_=tp[:].rearrange("p u j -> p j u"),
                    )
                else:
                    nc.scalar.copy(
                        out=gview[:, g, hf * 256:(hf + 1) * 256, :],
                        in_=tp[:].rearrange("p u j -> p j u"),
                    )

        def quant(loaded, codes, scales, g):
            raw, grouped = loaded
            nc.vector.quantize_mx(
                out=codes[:, g * 512:(g + 1) * 512].bitcast(FP8X4),
                scales=scales[:, g * 512:(g + 1) * 512],
                in_=grouped[:, g * 1024:(g + 1) * 1024].bitcast(BF16),
            )

        def prep(rows, codes, scales, pieces=1):
            loaded = prep_load(rows, pieces)
            turn(loaded, 0, 1)
            turn(loaded, 1, 2)
            quant(loaded, codes, scales, 0)
            quant(loaded, codes, scales, 1)

        def load_w(idx):
            m, c = divmod(idx, NCH)
            wcodes = stage.tile([P, 1024], U32, tag="wcodes", name="wcodes", align_bytes=64)
            wscales = stage.tile([P, 1024], U8, tag="wscales", name="wscales", align_bytes=64)
            loaded = prep_load(weights[m][c * CH:(c + 1) * CH, :], pieces=(2 if idx == 0 else 1))
            bbc = stage.tile([P, CH], BF16, tag="bbc", bufs=3, name="bbc")
            nc.sync.dma_start(out=bbc[:], in_=biases[m][c * CH:(c + 1) * CH].partition_broadcast(P))
            return loaded, (wcodes, wscales, bbc)

        def mx_rows(idx, ops, row_tiles):
            m, c = divmod(idx, NCH)
            wcodes, wscales, bbc = ops
            cols = slice(c * CH, (c + 1) * CH)
            for r in row_tiles:
                acc = psum.tile([P, CH], F32, tag="acc", name="acc")
                for g in range(2):
                    a_cols = slice(g * B + r * P, g * B + (r + 1) * P)
                    w_cols = slice(g * CH, (g + 1) * CH)
                    nc.tensor.matmul_mx(
                        out=acc[:],
                        lhsT=acodes[m][:, a_cols].bitcast(FP8X4),
                        lhsT_scale=ascales[m][:, a_cols],
                        rhs=wcodes[:, w_cols].bitcast(FP8X4),
                        rhs_scale=wscales[:, w_cols],
                        start=(g == 0),
                        stop=(g == 1),
                    )
                k = (m * RT + r) * NCH + c
                nc.vector.scalar_tensor_tensor(
                    out=va[m][:, r, cols], in0=acc[:], scalar=1.0, in1=bbc[:],
                    op0=ALU.mult, op1=ALU.add, accum_out=sums[:, k:k + 1],
                )

        def first_shift(idx):
            m, c = divmod(idx, NCH)
            if c == 0:
                first = sums[:, m * RT * NCH:(m + 1) * RT * NCH].rearrange("p (r c) -> p r c", c=NCH)[:, :, 0]
                nc.vector.tensor_scalar(
                    out=shift[m][:], in0=first, scalar1=-1.0 / CH, scalar2=None, op0=ALU.mult,
                )

        def squares(idx, row_tiles):
            m, c = divmod(idx, NCH)
            cols = slice(c * CH, (c + 1) * CH)
            for r in row_tiles:
                k = (m * RT + r) * NCH + c
                junk = stage.tile([P, CH], BF16, tag="junk", name="junk")
                nc.scalar.activation(
                    out=junk[:], in_=va[m][:, r, cols], func=ACT.Square,
                    bias=shift[m][:, r:r + 1], scale=1.0, accum_out=sqs[:, k:k + 1],
                )

        def small(name):
            return const.tile([P, RT], F32, name=name)

        stat_std = [small("std_%d" % m) for m in range(2)]

        def stats_a(m):
            n = float(G4)
            seg = slice(m * RT * NCH, (m + 1) * RT * NCH)
            s1 = small("s1_%d" % m)
            nc.vector.tensor_reduce(out=s1[:], in_=sums[:, seg].rearrange("p (r c) -> p r c", c=NCH), axis=AX.X, op=ALU.add)
            q1 = small("q1_%d" % m)
            nc.vector.tensor_reduce(out=q1[:], in_=sqs[:, seg].rearrange("p (r c) -> p r c", c=NCH), axis=AX.X, op=ALU.add)
            nc.vector.tensor_scalar(out=negmean[m][:], in0=s1[:], scalar1=-1.0 / n, scalar2=None, op0=ALU.mult)
            d = small("d_%d" % m)
            nc.vector.tensor_tensor(out=d[:], in0=shift[m][:], in1=negmean[m][:], op=ALU.subtract)
            d2 = small("d2_%d" % m)
            nc.vector.scalar_tensor_tensor(out=d2[:], in0=d[:], scalar=n, in1=d[:], op0=ALU.mult, op1=ALU.mult)
            var = small("var_%d" % m)
            nc.vector.tensor_tensor(out=var[:], in0=q1[:], in1=d2[:], op=ALU.subtract)
            nc.vector.tensor_scalar(out=var[:], in0=var[:], scalar1=1.0 / (n - 1.0), scalar2=0.0, op0=ALU.mult, op1=ALU.max)
            nc.gpsimd.tensor_tensor(out=stat_std[m][:], in0=var[:], in1=half[:], op=ALU.pow)

        def stats_b(m):
            std = stat_std[m]
            nc.vector.tensor_scalar(out=std[:], in0=std[:], scalar1=EPS, scalar2=None, op0=ALU.add)
            nc.vector.reciprocal(out=rinv[m][:], in_=std[:])
            nc.vector.tensor_tensor(out=nbias[m][:], in0=negmean[m][:], in1=rinv[m][:], op=ALU.mult)

        def norm(m, gate, on_scalar):
            cols = slice(gate * H, (gate + 1) * H)
            for r in range(RT):
                if r in on_scalar:
                    nc.scalar.activation(
                        out=va[m][:, r, cols], in_=va[m][:, r, cols], func=ACT.Identity,
                        scale=rinv[m][:, r:r + 1], bias=nbias[m][:, r:r + 1],
                    )
                else:
                    nc.vector.tensor_scalar(
                        out=va[m][:, r, cols], in0=va[m][:, r, cols],
                        scalar1=negmean[m][:, r:r + 1], scalar2=rinv[m][:, r:r + 1],
                        op0=ALU.add, op1=ALU.mult,
                    )

        def fa(q):
            for jt in range(4 * q, 4 * q + 4):
                cols = slice(jt * P, (jt + 1) * P)
                pf = psum.tile([P, RT, P], F32, tag="tp", name="pf")
                for r in range(RT):
                    nc.tensor.transpose(pf[:, r, :], va[0][:, r, cols], ident_f[:])
                nc.scalar.activation(
                    out=va[0][:, :, cols], in_=pf[:], func=ACT.Identity,
                    scale=vcf[:, jt:jt + 1], bias=lbc[:, jt:jt + 1],
                )

        def fb(q):
            for jt in range(4 * q, 4 * q + 4):
                cols = slice(jt * P, (jt + 1) * P)
                pf = psum.tile([P, RT, P], F32, tag="tp", name="pf")
                for r in range(RT):
                    nc.tensor.transpose(pf[:, r, :], va[1][:, r, cols], ident_f[:])
                nc.vector.scalar_tensor_tensor(
                    out=va[0][:, :, cols], in0=pf[:], scalar=vcf[:, 32 + jt:33 + jt], in1=va[0][:, :, cols],
                    op0=ALU.mult, op1=ALU.add,
                )

        def bphase(q):
            gate = q // 2
            cols = slice(q * CH, (q + 1) * CH)
            for r in range(RT):
                pb = psum.tile([P, CH], F32, tag="acc", name="pb")
                for t in range(4):
                    jt = 4 * q + t
                    nc.tensor.transpose(pb[:, t * P:(t + 1) * P], va[0][:, r, jt * P:(jt + 1) * P], ident_f[:])
                if gate == 1:
                    nc.scalar.activation(out=va[1][:, r, cols], in_=pb[:], func=ACT.Sigmoid, bias=negone[:, 0:1], scale=1.0)
                elif gate == 3:
                    nc.scalar.activation(out=va[1][:, r, cols], in_=pb[:], func=ACT.Tanh)
                else:
                    nc.scalar.activation(out=va[1][:, r, cols], in_=pb[:], func=ACT.Sigmoid)

        with tc.manual_schedule():
            prep(acts[0], acodes[0], ascales[0], pieces=4)
            loaded, nxt = load_w(0)
            turn(loaded, 0, 1)
            turn(loaded, 1, 2)
            quant(loaded, nxt[0], nxt[1], 0)
            quant(loaded, nxt[0], nxt[1], 1)
            for idx in range(2 * NCH):
                cur = nxt
                if idx == NCH - 2:
                    prep(acts[1], acodes[1], ascales[1])
                if idx == NCH + 2:
                    nc.sync.dma_start(out=cx_sb[:], in_=cx.rearrange("(r p) h -> p r h", p=P))
                    nc.sync.dma_start(out=w3bc[:], in_=ln_h2o_w.rearrange("o n -> (o n)").partition_broadcast(P))
                    nc.sync.dma_start(out=b3bc[:], in_=ln_h2o_b.rearrange("o n -> (o n)").partition_broadcast(P))
                more = idx + 1 < 2 * NCH
                if more:
                    loaded, nxt = load_w(idx + 1)
                    turn(loaded, 0, 1)
                if idx >= 1:
                    squares(idx - 1, (0, 1))
                mx_rows(idx, cur, (0, 1))
                if more:
                    quant(loaded, nxt[0], nxt[1], 0)
                    turn(loaded, 1, 2)
                if idx >= 1:
                    squares(idx - 1, (2, 3))
                mx_rows(idx, cur, (2, 3))
                if more:
                    quant(loaded, nxt[0], nxt[1], 1)
                first_shift(idx)
                if idx == 2:
                    vecs()
                if idx == NCH + 1:
                    stats_a(0)
                if idx == NCH + 2:
                    stats_b(0)
                if idx in (NCH + 3, NCH + 5):
                    norm(0, (1, 0)[(idx - NCH - 3) // 2], (3,))
            squares(2 * NCH - 1, (0, 1, 2, 3))
        fa(2)
        fa(0)
        stats_a(1)
        norm(0, 3, (3,))
        fa(6)
        stats_b(1)

        s3 = const.tile([P, RT], F32, name="s3")
        q3 = const.tile([P, RT], F32, name="q3")
        negm3 = const.tile([P, RT], F32, name="negm3")
        r3 = const.tile([P, RT], F32, name="r3")

        def parts(r):
            return (va[1][:, r, 0:H], va[1][:, r, H:2 * H], va[1][:, r, 2 * H:3 * H], va[1][:, r, 3 * H:4 * H],
                    va[0][:, r, 0:H], va[0][:, r, H:2 * H], va[0][:, r, 3 * H:4 * H], va[0][:, r, 2 * H:3 * H])

        s3h = const.tile([P, RT, 2], F32, name="s3h")

        def cab(hf):
            cc = slice(hf * CH, (hf + 1) * CH)
            for r in range(RT):
                gi, gf, go, gc, t0, t1, cn, hn = parts(r)
                nc.vector.tensor_tensor(out=t0[:, cc], in0=gf[:, cc], in1=cx_sb[:, r, cc], op=ALU.mult)
                nc.vector.tensor_tensor(out=t1[:, cc], in0=gi[:, cc], in1=gc[:, cc], op=ALU.mult)
                nc.vector.scalar_tensor_tensor(
                    out=cn[:, cc], in0=t0[:, cc], scalar=1.0, in1=t1[:, cc], op0=ALU.mult, op1=ALU.add,
                    accum_out=s3h[:, r, hf:hf + 1],
                )

        def c3(r):
            gi, gf, go, gc, t0, t1, cn, hn = parts(r)
            rr = slice(r, r + 1)
            nc.sync.dma_start(out=out_1[r * P:(r + 1) * P, :], in_=cn)
            nc.vector.tensor_tensor(out=s3[:, rr], in0=s3h[:, r, 0:1], in1=s3h[:, r, 1:2], op=ALU.add)
            nc.vector.tensor_scalar(out=negm3[:, rr], in0=s3[:, rr], scalar1=-1.0 / H, scalar2=None, op0=ALU.mult)
            nc.scalar.activation(out=t0, in_=cn, func=ACT.Square, bias=negm3[:, rr], scale=1.0, accum_out=q3[:, rr])
            nc.vector.scalar_tensor_tensor(out=t1, in0=cn, scalar=negm3[:, rr], in1=w3bc[:], op0=ALU.add, op1=ALU.mult)

        var3s = [const.tile([P, 1], F32, name="var3_%d" % r) for r in range(RT)]
        std3s = [const.tile([P, 1], F32, name="std3_%d" % r) for r in range(RT)]

        def fin1a(r):
            rr = slice(r, r + 1)
            nc.vector.tensor_scalar(out=var3s[r][:], in0=q3[:, rr], scalar1=1.0 / (H - 1.0), scalar2=None, op0=ALU.mult)
            nc.gpsimd.tensor_tensor(out=std3s[r][:], in0=var3s[r][:], in1=half[:, 0:1], op=ALU.pow)

        def fin1b(r):
            gi, gf, go, gc, t0, t1, cn, hn = parts(r)
            rr = slice(r, r + 1)
            var3 = var3s[r]
            std3 = std3s[r]
            nc.vector.tensor_scalar(out=var3[:], in0=std3[:], scalar1=EPS, scalar2=None, op0=ALU.add)
            nc.vector.reciprocal(out=r3[:, rr], in_=var3[:])
            nc.vector.scalar_tensor_tensor(out=t1, in0=t1, scalar=r3[:, rr], in1=b3bc[:], op0=ALU.mult, op1=ALU.add)
            nc.scalar.activation(out=t1, in_=t1, func=ACT.Tanh)

        def fin2(r):
            gi, gf, go, gc, t0, t1, cn, hn = parts(r)
            nc.vector.tensor_tensor(out=hn, in0=go, in1=t1, op=ALU.mult)
            nc.sync.dma_start(out=out_0[r * P:(r + 1) * P, :], in_=hn)

        norm(1, 1, (2, 3))
        norm(1, 0, (2, 3))
        fb(2)
        norm(1, 3, (2, 3))
        fb(0)
        bphase(2)
        fb(6)
        bphase(0)
        norm(0, 2, (3,))
        fa(3)
        fb(3)
        bphase(6)
        cab(0)
        fa(1)
        fb(1)
        bphase(3)
        norm(1, 2, (3,))
        fa(7)
        fb(7)
        bphase(1)
        fa(4)
        fb(4)
        bphase(7)
        cab(1)
        fa(5)
        fb(5)
        c3(0)
        c3(1)
        fin1a(0)
        bphase(4)
        c3(2)
        fin1a(1)
        fin1b(0)
        c3(3)
        fin1a(2)
        fin1b(1)
        bphase(5)
        fin2(0)
        fin1a(3)
        fin1b(2)
        fin2(1)
        fin1b(3)
        fin2(2)
        fin2(3)
